import numpy as np
import ml_dtypes


def mxq(x, axis, fmt="e4m3"):
    dtype, down = {"e4m3": (ml_dtypes.float8_e4m3fn, 7), "e5m2": (ml_dtypes.float8_e5m2, 14)}[fmt]
    v = np.moveaxis(np.asarray(x, np.float32).astype(ml_dtypes.bfloat16).astype(np.float64), axis, -1)
    blocks = v.reshape(v.shape[:-1] + (-1, 32))
    amax = np.abs(blocks).max(-1, keepdims=True)
    byte = np.maximum(np.where(amax > 0, np.frexp(amax)[1] - 1 + 127, 0) - down, 1)
    scale = np.exp2(byte - 127.0)
    codes = (blocks / scale).astype(np.float32).astype(dtype).astype(np.float64)
    return np.moveaxis((codes * scale).reshape(v.shape), -1, axis)


WIDE = False


def mx_kscale(k):
    if not WIDE:
        return np.ones(k)
    levels = np.array([20, -20, 10, -10, 0])
    a = np.random.permutation(np.resize(levels, k // 512 * 4)).reshape(k // 512, 4)
    idx = np.arange(k)
    return np.exp2(a[idx // 512, idx % 128 // 32])


BF16 = ml_dtypes.bfloat16


def bf(x):
    return np.asarray(x, np.float32).astype(BF16)


def f64(x):
    return np.asarray(x).astype(np.float64)


B, IN_F, OUT_F, N_ACT = 2048, 1024, 1024, 4


def sigmoid(v):
    return 1.0 / (1.0 + np.exp(-v))


def _cyclic_act_derivs(y):
    Bb, O = y.shape
    yg = y.reshape(Bb, O // N_ACT, N_ACT)
    th = np.tanh(yg[..., 0])
    sg = sigmoid(yg[..., 3])
    d = np.stack([
        1.0 - th * th,
        np.cos(yg[..., 1]),
        np.where(yg[..., 2] > 0.0, 1.0, 0.0),
        sg * (1.0 - sg),
    ], axis=-1)
    return d.reshape(Bb, O)


def setup_inputs():
    s = mx_kscale(B)[:, None]
    limit = np.sqrt(6.0 / (IN_F + OUT_F))
    x0 = bf(np.random.standard_normal((B, IN_F)))
    W = bf(np.random.uniform(-limit, limit, (OUT_F, IN_F)))
    b = bf(np.random.standard_normal(OUT_F) * 0.1)
    g = bf(np.random.standard_normal((B, OUT_F)) * np.exp2(np.random.randint(-12, 1, (B, 1))) / s)
    y = f64(x0) @ f64(W).T + f64(b)
    return {"input": bf(f64(x0) * s), "W": W, "b": b, "y": np.asarray(y, np.float32), "grad_out": g}


def reference(input, W, b, y, grad_out):
    dy = f64(grad_out) * _cyclic_act_derivs(f64(y))
    return mxq(dy, 0, "e5m2").T @ mxq(f64(input), 0, "e4m3")

@@ -1,0 +1,178 @@
+import math
+from contextlib import ExitStack
+
+import concourse.mybir as mybir
+
+F32 = mybir.dt.float32
+BF16 = mybir.dt.bfloat16
+U32 = mybir.dt.uint32
+U8 = mybir.dt.uint8
+E4M3X4 = mybir.dt.float8_e4m3fn_x4
+E5M2X4 = mybir.dt.float8_e5m2_x4
+ACT = mybir.ActivationFunctionType
+ALU = mybir.AluOpType
+
+TOKENS, IN_F, OUT_F, KINDS = 2048, 1024, 1024, 4
+
+P = 128
+PACK = 4
+K_PASS = P * PACK
+PASSES = TOKENS // K_PASS
+N_TILE = 512
+N_TILES = IN_F // N_TILE
+HALVES = 2
+HALF = OUT_F // HALVES
+M = HALF // KINDS
+assert M == P
+
+X_VECTOR_COLS = 512
+
+SIGN = (-1.0, 1.0, 1.0, -1.0)
+
+ROUND_MAGIC = 12582912.0
+
+FLOPS = 2 * TOKENS * IN_F * OUT_F
+BYTES = 2 * TOKENS * IN_F + (4 + 2) * TOKENS * OUT_F + 4 * OUT_F * IN_F
+
+
+def tile_vdl_v_kernel(tc, x, w, b, y, grad_out, out):
+    nc = tc.nc
+
+    x_rows = x.rearrange("(c p j) i -> c p j i", p=P, j=PACK)
+    y_rows = y.rearrange("(c p j) (h o) -> h c p j o", p=P, j=PACK, h=HALVES)
+    g_rows = grad_out.rearrange("(c p j) (h o) -> h c p j o", p=P, j=PACK, h=HALVES)
+    out_rows = out.rearrange("(h m kind) i -> h kind m i", h=HALVES, kind=KINDS)
+
+    with ExitStack() as ctx:
+        keep = ctx.enter_context(tc.tile_pool(name="keep", bufs=1))
+        x_pool = ctx.enter_context(tc.tile_pool(name="x_in", bufs=3))
+        xg_pool = ctx.enter_context(tc.tile_pool(name="x_grouped", bufs=2))
+        yg_pool = ctx.enter_context(tc.tile_pool(name="y_g_in", bufs=5))
+        work = ctx.enter_context(tc.tile_pool(name="work", bufs=3))
+        dy_pool = ctx.enter_context(tc.tile_pool(name="dy", bufs=3))
+        stage = ctx.enter_context(tc.tile_pool(name="stage", bufs=8))
+        psum = ctx.enter_context(tc.psum_pool(name="acc", bufs=1))
+
+        zero = keep.tile([P, 1], F32)
+        unused = keep.tile([P, 1], F32)
+        nc.vector.memset(zero[:], 0.0)
+        nc.scalar.activation(out=unused[:], in_=zero[:], func=ACT.Silu)
+
+        x_codes = keep.tile([P, PASSES, IN_F], U32, align_bytes=64)
+        x_scales = keep.tile([P, PASSES, IN_F], U8, align_bytes=64)
+
+        def quantise_x(c, x_raw, first, width, copy):
+            cols = slice(first, first + width)
+            grouped = xg_pool.tile(
+                [P, width, PACK], BF16, align_bytes=64, name="grouped", tag="grouped%d" % first
+            )
+            copy(
+                out=grouped[:].rearrange("p (r i) j -> p r j i", i=4),
+                in_=x_raw[:, :, cols].rearrange("p j (r i) -> p r j i", i=4),
+            )
+            nc.vector.quantize_mx(
+                out=x_codes[:, c, cols].bitcast(E4M3X4),
+                scales=x_scales[:, c, cols],
+                in_=grouped[:].rearrange("p col j -> p (col j)"),
+            )
+
+        def tanh_kind(dy_k, y_k, g_k, s, label):
+            th = work.tile([P, M, PACK], F32, name="th", tag="th" + label)
+            sq = work.tile([P, M, PACK], F32, name="sq", tag="sq" + label)
+            nc.scalar.activation(out=th[:], in_=y_k, func=ACT.Tanh, scale=s)
+            nc.scalar.activation(out=sq[:], in_=th[:], func=ACT.Square, scale=s)
+            nc.vector.scalar_tensor_tensor(
+                out=dy_k,
+                in0=sq[:],
+                scalar=s * s,
+                in1=g_k,
+                op0=ALU.subtract,
+                op1=ALU.mult,
+            )
+
+        def relu_kind(dy_k, y_k, g_k):
+            nc.vector.scalar_tensor_tensor(
+                out=dy_k, in0=y_k, scalar=0.0, in1=g_k, op0=ALU.is_gt, op1=ALU.mult
+            )
+
+        def sin_kind(dy_k, y_k, g_k):
+            turns = work.tile([P, M, PACK], F32)
+            whole = work.tile([P, M, PACK], F32)
+            frac = work.tile([P, M, PACK], F32)
+            cos_y = work.tile([P, M, PACK], F32)
+            nc.vector.tensor_scalar(
+                out=turns[:],
+                in0=y_k,
+                scalar1=1.0 / (2.0 * math.pi),
+                scalar2=0.25,
+                op0=ALU.mult,
+                op1=ALU.add,
+            )
+            nc.vector.tensor_scalar(
+                out=whole[:],
+                in0=turns[:],
+                scalar1=ROUND_MAGIC,
+                scalar2=ROUND_MAGIC,
+                op0=ALU.add,
+                op1=ALU.subtract,
+            )
+            nc.vector.tensor_tensor(out=frac[:], in0=turns[:], in1=whole[:], op=ALU.subtract)
+            nc.scalar.activation(out=cos_y[:], in_=frac[:], func=ACT.Sin, scale=2.0 * math.pi)
+            nc.vector.tensor_tensor(out=dy_k, in0=cos_y[:], in1=g_k, op=ALU.mult)
+
+        for h in range(HALVES):
+            acc = [
+                [psum.tile([P, N_TILE], F32, name="acc%d%d" % (kind, n)) for n in range(N_TILES)]
+                for kind in range(KINDS)
+            ]
+            for c in range(PASSES):
+                y_sb = yg_pool.tile([P, PACK, HALF], F32)
+                g_sb = yg_pool.tile([P, PACK, HALF], BF16)
+                nc.sync.dma_start(out=y_sb[:], in_=y_rows[h, c])
+                nc.sync.dma_start(out=g_sb[:], in_=g_rows[h, c])
+                y_kinds = y_sb[:].rearrange("p j (m kind) -> p kind m j", kind=KINDS)
+                g_kinds = g_sb[:].rearrange("p j (m kind) -> p kind m j", kind=KINDS)
+
+                dy = dy_pool.tile([P, KINDS, M, PACK], BF16, align_bytes=64)
+                dy_codes = dy_pool.tile([P, KINDS, M], U32, align_bytes=64)
+                dy_scales = dy_pool.tile([P, KINDS, M], U8, align_bytes=64)
+
+                relu_kind(dy[:, 2], y_kinds[:, 2], g_kinds[:, 2])
+                tanh_kind(dy[:, 0], y_kinds[:, 0], g_kinds[:, 0], 1.0, "_tanh")
+                tanh_kind(dy[:, 3], y_kinds[:, 3], g_kinds[:, 3], 0.5, "_sigmoid")
+                sin_kind(dy[:, 1], y_kinds[:, 1], g_kinds[:, 1])
+
+                if h == 0:
+                    x_raw = x_pool.tile([P, PACK, IN_F], BF16)
+                    nc.sync.dma_start(out=x_raw[:], in_=x_rows[c])
+                    quantise_x(c, x_raw, 0, X_VECTOR_COLS, nc.vector.tensor_copy)
+                    quantise_x(c, x_raw, X_VECTOR_COLS, IN_F - X_VECTOR_COLS, nc.scalar.copy)
+
+                for kind in (2, 0, 3, 1):
+                    nc.vector.quantize_mx(
+                        out=dy_codes[:, kind].bitcast(E5M2X4),
+                        scales=dy_scales[:, kind],
+                        in_=dy[:, kind].rearrange("p m j -> p (m j)"),
+                    )
+                    for n in range(N_TILES):
+                        n_cols = slice(n * N_TILE, (n + 1) * N_TILE)
+                        nc.tensor.matmul_mx(
+                            out=acc[kind][n][:],
+                            lhsT=dy_codes[:, kind].bitcast(E5M2X4),
+                            lhsT_scale=dy_scales[:, kind],
+                            rhs=x_codes[:, c, n_cols].bitcast(E4M3X4),
+                            rhs_scale=x_scales[:, c, n_cols],
+                            start=(c == 0),
+                            stop=(c == PASSES - 1),
+                        )
+
+            for kind in (2, 0, 3, 1):
+                result = stage.tile([P, IN_F], F32)
+                nc.scalar.mul(out=result[:, 0:N_TILE], in_=acc[kind][0][:], mul=SIGN[kind])
+                if h == HALVES - 1:
+                    nc.vector.tensor_scalar_mul(
+                        out=result[:, N_TILE:IN_F], in0=acc[kind][1][:], scalar1=SIGN[kind]
+                    )
+                else:
+                    nc.scalar.mul(out=result[:, N_TILE:IN_F], in_=acc[kind][1][:], mul=SIGN[kind])
+                nc.sync.dma_start(out=out_rows[h, kind], in_=result[:])

@@ -24,10 +24,13 @@ HALVES = 2
 HALF = OUT_F // HALVES
 M = HALF // KINDS
 assert M == P
+CHUNKS = HALVES * PASSES
+CHUNKS_AHEAD = 4
 
 X_VECTOR_COLS = 512
 
 SIGN = (-1.0, 1.0, 1.0, -1.0)
+LAST_KIND = 1
 
 ROUND_MAGIC = 12582912.0
 
@@ -45,134 +48,208 @@ def tile_vdl_v_kernel(tc, x, w, b, y, grad_out, out):
 
     with ExitStack() as ctx:
         keep = ctx.enter_context(tc.tile_pool(name="keep", bufs=1))
-        x_pool = ctx.enter_context(tc.tile_pool(name="x_in", bufs=3))
+        x_pool = ctx.enter_context(tc.tile_pool(name="x_in", bufs=PASSES))
         xg_pool = ctx.enter_context(tc.tile_pool(name="x_grouped", bufs=2))
-        yg_pool = ctx.enter_context(tc.tile_pool(name="y_g_in", bufs=5))
+        yg_pool = ctx.enter_context(tc.tile_pool(name="y_g_in", bufs=CHUNKS_AHEAD + 1))
         work = ctx.enter_context(tc.tile_pool(name="work", bufs=3))
         dy_pool = ctx.enter_context(tc.tile_pool(name="dy", bufs=3))
-        stage = ctx.enter_context(tc.tile_pool(name="stage", bufs=8))
+        stage = ctx.enter_context(tc.tile_pool(name="stage", bufs=KINDS))
         psum = ctx.enter_context(tc.psum_pool(name="acc", bufs=1))
-
-        zero = keep.tile([P, 1], F32)
-        unused = keep.tile([P, 1], F32)
-        nc.vector.memset(zero[:], 0.0)
-        nc.scalar.activation(out=unused[:], in_=zero[:], func=ACT.Silu)
+        ctx.enter_context(tc.manual_schedule())
 
         x_codes = keep.tile([P, PASSES, IN_F], U32, align_bytes=64)
         x_scales = keep.tile([P, PASSES, IN_F], U8, align_bytes=64)
 
-        def quantise_x(c, x_raw, first, width, copy):
-            cols = slice(first, first + width)
-            grouped = xg_pool.tile(
-                [P, width, PACK], BF16, align_bytes=64, name="grouped", tag="grouped%d" % first
-            )
-            copy(
-                out=grouped[:].rearrange("p (r i) j -> p r j i", i=4),
-                in_=x_raw[:, :, cols].rearrange("p j (r i) -> p r j i", i=4),
-            )
-            nc.vector.quantize_mx(
-                out=x_codes[:, c, cols].bitcast(E4M3X4),
-                scales=x_scales[:, c, cols],
-                in_=grouped[:].rearrange("p col j -> p (col j)"),
-            )
+        def load(i):
+            h, c = divmod(i, PASSES)
+            y_sb = yg_pool.tile([P, PACK, HALF], F32)
+            g_sb = yg_pool.tile([P, PACK, HALF], BF16)
+            nc.sync.dma_start(out=y_sb[:], in_=y_rows[h, c])
+            nc.sync.dma_start(out=g_sb[:], in_=g_rows[h, c])
+            tiles = {
+                "y": y_sb[:].rearrange("p j (m kind) -> p kind m j", kind=KINDS),
+                "g": g_sb[:].rearrange("p j (m kind) -> p kind m j", kind=KINDS),
+            }
+            if h == 0:
+                x_raw = x_pool.tile([P, PACK, IN_F], BF16)
+                nc.sync.dma_start(out=x_raw[:], in_=x_rows[c])
+                tiles["x"] = x_raw
+            return tiles
 
-        def tanh_kind(dy_k, y_k, g_k, s, label):
-            th = work.tile([P, M, PACK], F32, name="th", tag="th" + label)
-            sq = work.tile([P, M, PACK], F32, name="sq", tag="sq" + label)
-            nc.scalar.activation(out=th[:], in_=y_k, func=ACT.Tanh, scale=s)
-            nc.scalar.activation(out=sq[:], in_=th[:], func=ACT.Square, scale=s)
-            nc.vector.scalar_tensor_tensor(
-                out=dy_k,
-                in0=sq[:],
-                scalar=s * s,
-                in1=g_k,
-                op0=ALU.subtract,
-                op1=ALU.mult,
-            )
+        def tanh(tiles, kind, s):
+            th = work.tile([P, M, PACK], F32, name="th", tag="th%d" % kind)
+            nc.scalar.activation(out=th[:], in_=tiles["y"][:, kind], func=ACT.Tanh, scale=s)
+            tiles["th", kind] = th
 
-        def relu_kind(dy_k, y_k, g_k):
-            nc.vector.scalar_tensor_tensor(
-                out=dy_k, in0=y_k, scalar=0.0, in1=g_k, op0=ALU.is_gt, op1=ALU.mult
-            )
+        def square(tiles, kind, s):
+            sq = work.tile([P, M, PACK], F32, name="sq", tag="sq%d" % kind)
+            nc.scalar.activation(out=sq[:], in_=tiles["th", kind][:], func=ACT.Square, scale=s)
+            tiles["sq", kind] = sq
 
-        def sin_kind(dy_k, y_k, g_k):
-            turns = work.tile([P, M, PACK], F32)
-            whole = work.tile([P, M, PACK], F32)
-            frac = work.tile([P, M, PACK], F32)
-            cos_y = work.tile([P, M, PACK], F32)
+        def turns(tiles, kind):
+            t = work.tile([P, M, PACK], F32, name="turns")
             nc.vector.tensor_scalar(
-                out=turns[:],
-                in0=y_k,
+                out=t[:],
+                in0=tiles["y"][:, kind],
                 scalar1=1.0 / (2.0 * math.pi),
                 scalar2=0.25,
                 op0=ALU.mult,
                 op1=ALU.add,
             )
+            tiles["turns"] = t
+
+        def whole_turns(tiles):
+            whole = work.tile([P, M, PACK], F32)
             nc.vector.tensor_scalar(
                 out=whole[:],
-                in0=turns[:],
+                in0=tiles["turns"][:],
                 scalar1=ROUND_MAGIC,
                 scalar2=ROUND_MAGIC,
                 op0=ALU.add,
                 op1=ALU.subtract,
             )
-            nc.vector.tensor_tensor(out=frac[:], in0=turns[:], in1=whole[:], op=ALU.subtract)
+            tiles["whole"] = whole
+
+        def cosine(tiles):
+            frac = work.tile([P, M, PACK], F32)
+            cos_y = work.tile([P, M, PACK], F32)
+            nc.vector.tensor_tensor(
+                out=frac[:], in0=tiles["turns"][:], in1=tiles["whole"][:], op=ALU.subtract
+            )
             nc.scalar.activation(out=cos_y[:], in_=frac[:], func=ACT.Sin, scale=2.0 * math.pi)
-            nc.vector.tensor_tensor(out=dy_k, in0=cos_y[:], in1=g_k, op=ALU.mult)
+            tiles["cos"] = cos_y
 
-        for h in range(HALVES):
-            acc = [
-                [psum.tile([P, N_TILE], F32, name="acc%d%d" % (kind, n)) for n in range(N_TILES)]
-                for kind in range(KINDS)
-            ]
-            for c in range(PASSES):
-                y_sb = yg_pool.tile([P, PACK, HALF], F32)
-                g_sb = yg_pool.tile([P, PACK, HALF], BF16)
-                nc.sync.dma_start(out=y_sb[:], in_=y_rows[h, c])
-                nc.sync.dma_start(out=g_sb[:], in_=g_rows[h, c])
-                y_kinds = y_sb[:].rearrange("p j (m kind) -> p kind m j", kind=KINDS)
-                g_kinds = g_sb[:].rearrange("p j (m kind) -> p kind m j", kind=KINDS)
+        def group_x(tiles, first, width, copy):
+            grouped = xg_pool.tile(
+                [P, width, PACK], BF16, align_bytes=64, name="grouped", tag="grouped%d" % first
+            )
+            copy(
+                out=grouped[:].rearrange("p (r i) j -> p r j i", i=4),
+                in_=tiles["x"][:, :, first : first + width].rearrange("p j (r i) -> p r j i", i=4),
+            )
+            tiles["grouped", first] = grouped
 
-                dy = dy_pool.tile([P, KINDS, M, PACK], BF16, align_bytes=64)
-                dy_codes = dy_pool.tile([P, KINDS, M], U32, align_bytes=64)
-                dy_scales = dy_pool.tile([P, KINDS, M], U8, align_bytes=64)
+        def quantise_x(tiles, c, first, width):
+            cols = slice(first, first + width)
+            nc.vector.quantize_mx(
+                out=x_codes[:, c, cols].bitcast(E4M3X4),
+                scales=x_scales[:, c, cols],
+                in_=tiles["grouped", first][:].rearrange("p col j -> p (col j)"),
+            )
 
-                relu_kind(dy[:, 2], y_kinds[:, 2], g_kinds[:, 2])
-                tanh_kind(dy[:, 0], y_kinds[:, 0], g_kinds[:, 0], 1.0, "_tanh")
-                tanh_kind(dy[:, 3], y_kinds[:, 3], g_kinds[:, 3], 0.5, "_sigmoid")
-                sin_kind(dy[:, 1], y_kinds[:, 1], g_kinds[:, 1])
+        def times_grad_relu(tiles, kind):
+            nc.vector.scalar_tensor_tensor(
+                out=tiles["dy"][:, kind],
+                in0=tiles["y"][:, kind],
+                scalar=0.0,
+                in1=tiles["g"][:, kind],
+                op0=ALU.is_gt,
+                op1=ALU.mult,
+            )
 
-                if h == 0:
-                    x_raw = x_pool.tile([P, PACK, IN_F], BF16)
-                    nc.sync.dma_start(out=x_raw[:], in_=x_rows[c])
-                    quantise_x(c, x_raw, 0, X_VECTOR_COLS, nc.vector.tensor_copy)
-                    quantise_x(c, x_raw, X_VECTOR_COLS, IN_F - X_VECTOR_COLS, nc.scalar.copy)
+        def times_grad_tanh(tiles, kind, s):
+            nc.vector.scalar_tensor_tensor(
+                out=tiles["dy"][:, kind],
+                in0=tiles["sq", kind][:],
+                scalar=s * s,
+                in1=tiles["g"][:, kind],
+                op0=ALU.subtract,
+                op1=ALU.mult,
+            )
 
-                for kind in (2, 0, 3, 1):
-                    nc.vector.quantize_mx(
-                        out=dy_codes[:, kind].bitcast(E5M2X4),
-                        scales=dy_scales[:, kind],
-                        in_=dy[:, kind].rearrange("p m j -> p (m j)"),
-                    )
-                    for n in range(N_TILES):
-                        n_cols = slice(n * N_TILE, (n + 1) * N_TILE)
-                        nc.tensor.matmul_mx(
-                            out=acc[kind][n][:],
-                            lhsT=dy_codes[:, kind].bitcast(E5M2X4),
-                            lhsT_scale=dy_scales[:, kind],
-                            rhs=x_codes[:, c, n_cols].bitcast(E4M3X4),
-                            rhs_scale=x_scales[:, c, n_cols],
-                            start=(c == 0),
-                            stop=(c == PASSES - 1),
-                        )
+        def times_grad_cos(tiles, kind):
+            nc.vector.tensor_tensor(
+                out=tiles["dy"][:, kind], in0=tiles["cos"][:], in1=tiles["g"][:, kind], op=ALU.mult
+            )
 
-            for kind in (2, 0, 3, 1):
+        def multiply(tiles, i, kind, acc):
+            h, c = divmod(i, PASSES)
+            nc.vector.quantize_mx(
+                out=tiles["codes"][:, kind].bitcast(E5M2X4),
+                scales=tiles["scales"][:, kind],
+                in_=tiles["dy"][:, kind].rearrange("p m j -> p (m j)"),
+            )
+            for n in range(N_TILES):
+                n_cols = slice(n * N_TILE, (n + 1) * N_TILE)
+                nc.tensor.matmul_mx(
+                    out=acc[kind][n][:],
+                    lhsT=tiles["codes"][:, kind].bitcast(E5M2X4),
+                    lhsT_scale=tiles["scales"][:, kind],
+                    rhs=x_codes[:, c, n_cols].bitcast(E4M3X4),
+                    rhs_scale=x_scales[:, c, n_cols],
+                    start=(c == 0),
+                    stop=(c == PASSES - 1),
+                )
+            if c == PASSES - 1:
                 result = stage.tile([P, IN_F], F32)
                 nc.scalar.mul(out=result[:, 0:N_TILE], in_=acc[kind][0][:], mul=SIGN[kind])
-                if h == HALVES - 1:
+                if i == CHUNKS - 1 and kind == LAST_KIND:
                     nc.vector.tensor_scalar_mul(
                         out=result[:, N_TILE:IN_F], in0=acc[kind][1][:], scalar1=SIGN[kind]
                     )
                 else:
                     nc.scalar.mul(out=result[:, N_TILE:IN_F], in_=acc[kind][1][:], mul=SIGN[kind])
                 nc.sync.dma_start(out=out_rows[h, kind], in_=result[:])
+
+        zero = keep.tile([P, 1], F32)
+        unused = keep.tile([P, 1], F32)
+        nc.vector.memset(zero[:], 0.0)
+        nc.scalar.activation(out=unused[:], in_=zero[:], func=ACT.Silu)
+
+        chunks = {}
+        for i in range(CHUNKS_AHEAD):
+            chunks[i] = load(i)
+
+        acc = None
+        for r in range(-1, CHUNKS):
+            if 0 <= r and r + CHUNKS_AHEAD < CHUNKS:
+                chunks[r + CHUNKS_AHEAD] = load(r + CHUNKS_AHEAD)
+            old = chunks.get(r)
+            new = chunks.get(r + 1)
+            with_x = new is not None and "x" in new
+
+            if new is not None:
+                tanh(new, 0, 1.0)
+                tanh(new, 3, 0.5)
+                square(new, 0, 1.0)
+                square(new, 3, 0.5)
+            if with_x:
+                group_x(new, X_VECTOR_COLS, IN_F - X_VECTOR_COLS, nc.scalar.copy)
+
+            if old is not None:
+                if r % PASSES == 0:
+                    acc = [
+                        [
+                            psum.tile([P, N_TILE], F32, name="acc%d%d" % (kind, n))
+                            for n in range(N_TILES)
+                        ]
+                        for kind in range(KINDS)
+                    ]
+                old["dy"] = dy_pool.tile([P, KINDS, M, PACK], BF16, align_bytes=64, name="dy")
+                old["codes"] = dy_pool.tile([P, KINDS, M], U32, align_bytes=64, name="dy_codes")
+                old["scales"] = dy_pool.tile([P, KINDS, M], U8, align_bytes=64, name="dy_scales")
+
+            if old is not None:
+                times_grad_relu(old, 2)
+            if new is not None:
+                turns(new, 1)
+            if old is not None:
+                times_grad_tanh(old, 0, 1.0)
+                multiply(old, r, 2, acc)
+            if new is not None:
+                whole_turns(new)
+            if old is not None:
+                times_grad_tanh(old, 3, 0.5)
+                multiply(old, r, 0, acc)
+            if new is not None:
+                cosine(new)
+            if old is not None:
+                times_grad_cos(old, 1)
+                multiply(old, r, 3, acc)
+            if with_x:
+                group_x(new, 0, X_VECTOR_COLS, nc.vector.tensor_copy)
+            if old is not None:
+                multiply(old, r, LAST_KIND, acc)
+            if with_x:
+                quantise_x(new, r + 1, 0, X_VECTOR_COLS)
+                quantise_x(new, r + 1, X_VECTOR_COLS, IN_F - X_VECTOR_COLS)

@@ -51,7 +51,8 @@ def tile_vdl_v_kernel(tc, x, w, b, y, grad_out, out):
         x_pool = ctx.enter_context(tc.tile_pool(name="x_in", bufs=PASSES))
         xg_pool = ctx.enter_context(tc.tile_pool(name="x_grouped", bufs=2))
         yg_pool = ctx.enter_context(tc.tile_pool(name="y_g_in", bufs=CHUNKS_AHEAD + 1))
-        work = ctx.enter_context(tc.tile_pool(name="work", bufs=3))
+        work = ctx.enter_context(tc.tile_pool(name="work", bufs=2))
+        ready = ctx.enter_context(tc.tile_pool(name="ready", bufs=3))
         dy_pool = ctx.enter_context(tc.tile_pool(name="dy", bufs=3))
         stage = ctx.enter_context(tc.tile_pool(name="stage", bufs=KINDS))
         psum = ctx.enter_context(tc.psum_pool(name="acc", bufs=1))
@@ -68,7 +69,8 @@ def tile_vdl_v_kernel(tc, x, w, b, y, grad_out, out):
             nc.sync.dma_start(out=g_sb[:], in_=g_rows[h, c])
             tiles = {
                 "y": y_sb[:].rearrange("p j (m kind) -> p kind m j", kind=KINDS),
-                "g": g_sb[:].rearrange("p j (m kind) -> p kind m j", kind=KINDS),
+                "y23": y_sb[:].rearrange("p j (m pair e) -> p pair m j e", pair=2, e=2)[:, 1],
+                "g_raw": g_sb,
             }
             if h == 0:
                 x_raw = x_pool.tile([P, PACK, IN_F], BF16)
@@ -76,14 +78,22 @@ def tile_vdl_v_kernel(tc, x, w, b, y, grad_out, out):
                 tiles["x"] = x_raw
             return tiles
 
-        def tanh(tiles, kind, s):
-            th = work.tile([P, M, PACK], F32, name="th", tag="th%d" % kind)
-            nc.scalar.activation(out=th[:], in_=tiles["y"][:, kind], func=ACT.Tanh, scale=s)
-            tiles["th", kind] = th
+        def tanh_of_y(tiles):
+            th = work.tile([P, M, PACK], F32, name="th0")
+            nc.scalar.activation(out=th[:], in_=tiles["y"][:, 0], func=ACT.Tanh)
+            tiles["th", 0] = th[:]
+
+        def tanh_of_half_y(tiles):
+            th = ready.tile([P, 2, M, PACK], F32, name="th23")
+            nc.scalar.activation(
+                out=th[:].rearrange("p e m j -> p m j e"), in_=tiles["y23"], func=ACT.Tanh, scale=0.5
+            )
+            tiles["th", 2] = th[:, 0]
+            tiles["th", 3] = th[:, 1]
 
         def square(tiles, kind, s):
-            sq = work.tile([P, M, PACK], F32, name="sq", tag="sq%d" % kind)
-            nc.scalar.activation(out=sq[:], in_=tiles["th", kind][:], func=ACT.Square, scale=s)
+            sq = ready.tile([P, M, PACK], F32, name="sq", tag="sq%d" % kind)
+            nc.scalar.activation(out=sq[:], in_=tiles["th", kind], func=ACT.Square, scale=s)
             tiles["sq", kind] = sq
 
         def turns(tiles, kind):
@@ -112,21 +122,29 @@ def tile_vdl_v_kernel(tc, x, w, b, y, grad_out, out):
 
         def cosine(tiles):
             frac = work.tile([P, M, PACK], F32)
-            cos_y = work.tile([P, M, PACK], F32)
+            cos_y = ready.tile([P, M, PACK], F32)
             nc.vector.tensor_tensor(
                 out=frac[:], in0=tiles["turns"][:], in1=tiles["whole"][:], op=ALU.subtract
             )
             nc.scalar.activation(out=cos_y[:], in_=frac[:], func=ACT.Sin, scale=2.0 * math.pi)
             tiles["cos"] = cos_y
 
+        def group(copy, grouped, rows):
+            copy(
+                out=grouped.rearrange("p (r i) j -> p r j i", i=4),
+                in_=rows.rearrange("p j (r i) -> p r j i", i=4),
+            )
+
+        def group_g(tiles):
+            grouped = ready.tile([P, HALF, PACK], BF16, name="g_grouped")
+            group(nc.vector.tensor_copy, grouped[:], tiles["g_raw"][:])
+            tiles["g"] = grouped[:].rearrange("p (m kind) j -> p kind m j", kind=KINDS)
+
         def group_x(tiles, first, width, copy):
             grouped = xg_pool.tile(
                 [P, width, PACK], BF16, align_bytes=64, name="grouped", tag="grouped%d" % first
             )
-            copy(
-                out=grouped[:].rearrange("p (r i) j -> p r j i", i=4),
-                in_=tiles["x"][:, :, first : first + width].rearrange("p j (r i) -> p r j i", i=4),
-            )
+            group(copy, grouped[:], tiles["x"][:, :, first : first + width])
             tiles["grouped", first] = grouped
 
         def quantise_x(tiles, c, first, width):
@@ -140,7 +158,7 @@ def tile_vdl_v_kernel(tc, x, w, b, y, grad_out, out):
         def times_grad_relu(tiles, kind):
             nc.vector.scalar_tensor_tensor(
                 out=tiles["dy"][:, kind],
-                in0=tiles["y"][:, kind],
+                in0=tiles["th", kind],
                 scalar=0.0,
                 in1=tiles["g"][:, kind],
                 op0=ALU.is_gt,
@@ -209,8 +227,8 @@ def tile_vdl_v_kernel(tc, x, w, b, y, grad_out, out):
             with_x = new is not None and "x" in new
 
             if new is not None:
-                tanh(new, 0, 1.0)
-                tanh(new, 3, 0.5)
+                tanh_of_y(new)
+                tanh_of_half_y(new)
                 square(new, 0, 1.0)
                 square(new, 3, 0.5)
             if with_x:
@@ -250,6 +268,8 @@ def tile_vdl_v_kernel(tc, x, w, b, y, grad_out, out):
                 group_x(new, 0, X_VECTOR_COLS, nc.vector.tensor_copy)
             if old is not None:
                 multiply(old, r, LAST_KIND, acc)
+            if new is not None:
+                group_g(new)
             if with_x:
                 quantise_x(new, r + 1, 0, X_VECTOR_COLS)
                 quantise_x(new, r + 1, X_VECTOR_COLS, IN_F - X_VECTOR_COLS)

@@ -25,7 +25,7 @@ HALF = OUT_F // HALVES
 M = HALF // KINDS
 assert M == P
 CHUNKS = HALVES * PASSES
-CHUNKS_AHEAD = 4
+CHUNKS_AHEAD = 5
 
 X_VECTOR_COLS = 512
 
@@ -50,11 +50,11 @@ def tile_vdl_v_kernel(tc, x, w, b, y, grad_out, out):
         keep = ctx.enter_context(tc.tile_pool(name="keep", bufs=1))
         x_pool = ctx.enter_context(tc.tile_pool(name="x_in", bufs=PASSES))
         xg_pool = ctx.enter_context(tc.tile_pool(name="x_grouped", bufs=2))
-        yg_pool = ctx.enter_context(tc.tile_pool(name="y_g_in", bufs=CHUNKS_AHEAD + 1))
+        yg_pool = ctx.enter_context(tc.tile_pool(name="y_g_in", bufs=CHUNKS_AHEAD))
         work = ctx.enter_context(tc.tile_pool(name="work", bufs=2))
         ready = ctx.enter_context(tc.tile_pool(name="ready", bufs=3))
         dy_pool = ctx.enter_context(tc.tile_pool(name="dy", bufs=3))
-        stage = ctx.enter_context(tc.tile_pool(name="stage", bufs=KINDS))
+        stage = ctx.enter_context(tc.tile_pool(name="stage", bufs=KINDS * N_TILES))
         psum = ctx.enter_context(tc.psum_pool(name="acc", bufs=1))
         ctx.enter_context(tc.manual_schedule())
 
@@ -120,13 +120,18 @@ def tile_vdl_v_kernel(tc, x, w, b, y, grad_out, out):
             )
             tiles["whole"] = whole
 
-        def cosine(tiles):
-            frac = work.tile([P, M, PACK], F32)
-            cos_y = ready.tile([P, M, PACK], F32)
+        def part_of_a_turn(tiles):
+            frac = ready.tile([P, M, PACK], F32)
             nc.vector.tensor_tensor(
                 out=frac[:], in0=tiles["turns"][:], in1=tiles["whole"][:], op=ALU.subtract
             )
-            nc.scalar.activation(out=cos_y[:], in_=frac[:], func=ACT.Sin, scale=2.0 * math.pi)
+            tiles["frac"] = frac
+
+        def cosine(tiles):
+            cos_y = ready.tile([P, M, PACK], F32)
+            nc.scalar.activation(
+                out=cos_y[:], in_=tiles["frac"][:], func=ACT.Sin, scale=2.0 * math.pi
+            )
             tiles["cos"] = cos_y
 
         def group(copy, grouped, rows):
@@ -198,16 +203,15 @@ def tile_vdl_v_kernel(tc, x, w, b, y, grad_out, out):
                     start=(c == 0),
                     stop=(c == PASSES - 1),
                 )
-            if c == PASSES - 1:
-                result = stage.tile([P, IN_F], F32)
-                nc.scalar.mul(out=result[:, 0:N_TILE], in_=acc[kind][0][:], mul=SIGN[kind])
-                if i == CHUNKS - 1 and kind == LAST_KIND:
-                    nc.vector.tensor_scalar_mul(
-                        out=result[:, N_TILE:IN_F], in0=acc[kind][1][:], scalar1=SIGN[kind]
-                    )
-                else:
-                    nc.scalar.mul(out=result[:, N_TILE:IN_F], in_=acc[kind][1][:], mul=SIGN[kind])
-                nc.sync.dma_start(out=out_rows[h, kind], in_=result[:])
+                if c == PASSES - 1:
+                    result = stage.tile([P, N_TILE], F32)
+                    if i == CHUNKS - 1 and kind == LAST_KIND and n == N_TILES - 1:
+                        nc.vector.tensor_scalar_mul(
+                            out=result[:], in0=acc[kind][n][:], scalar1=SIGN[kind]
+                        )
+                    else:
+                        nc.scalar.mul(out=result[:], in_=acc[kind][n][:], mul=SIGN[kind])
+                    nc.sync.dma_start(out=out_rows[h, kind][:, n_cols], in_=result[:])
 
         zero = keep.tile([P, 1], F32)
         unused = keep.tile([P, 1], F32)
@@ -215,24 +219,22 @@ def tile_vdl_v_kernel(tc, x, w, b, y, grad_out, out):
         nc.scalar.activation(out=unused[:], in_=zero[:], func=ACT.Silu)
 
         chunks = {}
-        for i in range(CHUNKS_AHEAD):
-            chunks[i] = load(i)
-
         acc = None
-        for r in range(-1, CHUNKS):
-            if 0 <= r and r + CHUNKS_AHEAD < CHUNKS:
+        for r in range(-CHUNKS_AHEAD, CHUNKS):
+            if r + CHUNKS_AHEAD < CHUNKS:
                 chunks[r + CHUNKS_AHEAD] = load(r + CHUNKS_AHEAD)
             old = chunks.get(r)
             new = chunks.get(r + 1)
-            with_x = new is not None and "x" in new
+            far = chunks.get(r + 2)
 
             if new is not None:
                 tanh_of_y(new)
                 tanh_of_half_y(new)
                 square(new, 0, 1.0)
                 square(new, 3, 0.5)
-            if with_x:
-                group_x(new, X_VECTOR_COLS, IN_F - X_VECTOR_COLS, nc.scalar.copy)
+                cosine(new)
+                if "x" in new:
+                    group_x(new, X_VECTOR_COLS, IN_F - X_VECTOR_COLS, nc.scalar.copy)
 
             if old is not None:
                 if r % PASSES == 0:
@@ -248,28 +250,29 @@ def tile_vdl_v_kernel(tc, x, w, b, y, grad_out, out):
                 old["scales"] = dy_pool.tile([P, KINDS, M], U8, align_bytes=64, name="dy_scales")
 
             if old is not None:
+                if "x" in old:
+                    quantise_x(old, r, X_VECTOR_COLS, IN_F - X_VECTOR_COLS)
                 times_grad_relu(old, 2)
-            if new is not None:
-                turns(new, 1)
+                if "x" in old:
+                    quantise_x(old, r, 0, X_VECTOR_COLS)
+            if far is not None:
+                turns(far, 1)
             if old is not None:
                 times_grad_tanh(old, 0, 1.0)
                 multiply(old, r, 2, acc)
-            if new is not None:
-                whole_turns(new)
+            if far is not None:
+                whole_turns(far)
             if old is not None:
                 times_grad_tanh(old, 3, 0.5)
                 multiply(old, r, 0, acc)
-            if new is not None:
-                cosine(new)
+            if far is not None:
+                part_of_a_turn(far)
             if old is not None:
                 times_grad_cos(old, 1)
                 multiply(old, r, 3, acc)
-            if with_x:
-                group_x(new, 0, X_VECTOR_COLS, nc.vector.tensor_copy)
-            if old is not None:
-                multiply(old, r, LAST_KIND, acc)
             if new is not None:
                 group_g(new)
-            if with_x:
-                quantise_x(new, r + 1, 0, X_VECTOR_COLS)
-                quantise_x(new, r + 1, X_VECTOR_COLS, IN_F - X_VECTOR_COLS)
+            if old is not None:
+                multiply(old, r, LAST_KIND, acc)
+            if new is not None and "x" in new:
+                group_x(new, 0, X_VECTOR_COLS, nc.vector.tensor_copy)

@@ -25,9 +25,9 @@ HALF = OUT_F // HALVES
 M = HALF // KINDS
 assert M == P
 CHUNKS = HALVES * PASSES
-CHUNKS_AHEAD = 5
+CHUNKS_AHEAD = 4
 
-X_VECTOR_COLS = 512
+X_VECTOR_COLS = 384
 
 SIGN = (-1.0, 1.0, 1.0, -1.0)
 LAST_KIND = 1
@@ -50,7 +50,7 @@ def tile_vdl_v_kernel(tc, x, w, b, y, grad_out, out):
         keep = ctx.enter_context(tc.tile_pool(name="keep", bufs=1))
         x_pool = ctx.enter_context(tc.tile_pool(name="x_in", bufs=PASSES))
         xg_pool = ctx.enter_context(tc.tile_pool(name="x_grouped", bufs=2))
-        yg_pool = ctx.enter_context(tc.tile_pool(name="y_g_in", bufs=CHUNKS_AHEAD))
+        yg_pool = ctx.enter_context(tc.tile_pool(name="y_g_in", bufs=CHUNKS_AHEAD + 1))
         work = ctx.enter_context(tc.tile_pool(name="work", bufs=2))
         ready = ctx.enter_context(tc.tile_pool(name="ready", bufs=3))
         dy_pool = ctx.enter_context(tc.tile_pool(name="dy", bufs=3))
@@ -64,9 +64,8 @@ def tile_vdl_v_kernel(tc, x, w, b, y, grad_out, out):
         def load(i):
             h, c = divmod(i, PASSES)
             y_sb = yg_pool.tile([P, PACK, HALF], F32)
-            g_sb = yg_pool.tile([P, PACK, HALF], BF16)
+            g_sb = yg_pool.tile([P, PACK * HALF], BF16)
             nc.sync.dma_start(out=y_sb[:], in_=y_rows[h, c])
-            nc.sync.dma_start(out=g_sb[:], in_=g_rows[h, c])
             tiles = {
                 "y": y_sb[:].rearrange("p j (m kind) -> p kind m j", kind=KINDS),
                 "y23": y_sb[:].rearrange("p j (m pair e) -> p pair m j e", pair=2, e=2)[:, 1],
@@ -76,6 +75,7 @@ def tile_vdl_v_kernel(tc, x, w, b, y, grad_out, out):
                 x_raw = x_pool.tile([P, PACK, IN_F], BF16)
                 nc.sync.dma_start(out=x_raw[:], in_=x_rows[c])
                 tiles["x"] = x_raw
+            nc.sync.dma_start(out=g_sb[:].rearrange("p (j o) -> p j o", j=PACK), in_=g_rows[h, c])
             return tiles
 
         def tanh_of_y(tiles):
@@ -120,44 +120,37 @@ def tile_vdl_v_kernel(tc, x, w, b, y, grad_out, out):
             )
             tiles["whole"] = whole
 
-        def part_of_a_turn(tiles):
-            frac = ready.tile([P, M, PACK], F32)
+        def cosine(tiles):
+            frac = work.tile([P, M, PACK], F32)
+            cos_y = ready.tile([P, M, PACK], F32)
             nc.vector.tensor_tensor(
                 out=frac[:], in0=tiles["turns"][:], in1=tiles["whole"][:], op=ALU.subtract
             )
-            tiles["frac"] = frac
-
-        def cosine(tiles):
-            cos_y = ready.tile([P, M, PACK], F32)
-            nc.scalar.activation(
-                out=cos_y[:], in_=tiles["frac"][:], func=ACT.Sin, scale=2.0 * math.pi
-            )
+            nc.scalar.activation(out=cos_y[:], in_=frac[:], func=ACT.Sin, scale=2.0 * math.pi)
             tiles["cos"] = cos_y
 
-        def group(copy, grouped, rows):
-            copy(
-                out=grouped.rearrange("p (r i) j -> p r j i", i=4),
-                in_=rows.rearrange("p j (r i) -> p r j i", i=4),
-            )
-
         def group_g(tiles):
-            grouped = ready.tile([P, HALF, PACK], BF16, name="g_grouped")
-            group(nc.vector.tensor_copy, grouped[:], tiles["g_raw"][:])
-            tiles["g"] = grouped[:].rearrange("p (m kind) j -> p kind m j", kind=KINDS)
-
-        def group_x(tiles, first, width, copy):
-            grouped = xg_pool.tile(
-                [P, width, PACK], BF16, align_bytes=64, name="grouped", tag="grouped%d" % first
+            words = ready.tile([P, PACK * HALF], BF16, name="g_words")
+            nc.vector.tensor_copy(
+                out=words[:].bitcast(F32).rearrange("p (pair j) -> p pair j", j=PACK),
+                in_=tiles["g_raw"][:].bitcast(F32).rearrange("p (j pair) -> p pair j", j=PACK),
             )
-            group(copy, grouped[:], tiles["x"][:, :, first : first + width])
-            tiles["grouped", first] = grouped
+            by_kind = words[:].rearrange("p (m hi j lo) -> p hi lo m j", hi=2, j=PACK, lo=2)
+            for kind in range(KINDS):
+                tiles["g", kind] = by_kind[:, kind // 2, kind % 2]
 
-        def quantise_x(tiles, c, first, width):
-            cols = slice(first, first + width)
+        def group_x(tiles, first, last, copy):
+            copy(
+                out=tiles["x_grouped"][:, first:last, :].rearrange("p (r i) j -> p r j i", i=4),
+                in_=tiles["x"][:, :, first:last].rearrange("p j (r i) -> p r j i", i=4),
+            )
+
+        def quantise_x(tiles, c, n):
+            n_cols = slice(n * N_TILE, (n + 1) * N_TILE)
             nc.vector.quantize_mx(
-                out=x_codes[:, c, cols].bitcast(E4M3X4),
-                scales=x_scales[:, c, cols],
-                in_=tiles["grouped", first][:].rearrange("p col j -> p (col j)"),
+                out=x_codes[:, c, n_cols].bitcast(E4M3X4),
+                scales=x_scales[:, c, n_cols],
+                in_=tiles["x_grouped"][:, n_cols, :].rearrange("p col j -> p (col j)"),
             )
 
         def times_grad_relu(tiles, kind):
@@ -165,7 +158,7 @@ def tile_vdl_v_kernel(tc, x, w, b, y, grad_out, out):
                 out=tiles["dy"][:, kind],
                 in0=tiles["th", kind],
                 scalar=0.0,
-                in1=tiles["g"][:, kind],
+                in1=tiles["g", kind],
                 op0=ALU.is_gt,
                 op1=ALU.mult,
             )
@@ -175,14 +168,14 @@ def tile_vdl_v_kernel(tc, x, w, b, y, grad_out, out):
                 out=tiles["dy"][:, kind],
                 in0=tiles["sq", kind][:],
                 scalar=s * s,
-                in1=tiles["g"][:, kind],
+                in1=tiles["g", kind],
                 op0=ALU.subtract,
                 op1=ALU.mult,
             )
 
         def times_grad_cos(tiles, kind):
             nc.vector.tensor_tensor(
-                out=tiles["dy"][:, kind], in0=tiles["cos"][:], in1=tiles["g"][:, kind], op=ALU.mult
+                out=tiles["dy"][:, kind], in0=tiles["cos"][:], in1=tiles["g", kind], op=ALU.mult
             )
 
         def multiply(tiles, i, kind, acc):
@@ -219,22 +212,26 @@ def tile_vdl_v_kernel(tc, x, w, b, y, grad_out, out):
         nc.scalar.activation(out=unused[:], in_=zero[:], func=ACT.Silu)
 
         chunks = {}
+        for i in range(CHUNKS_AHEAD):
+            chunks[i] = load(i)
+
         acc = None
-        for r in range(-CHUNKS_AHEAD, CHUNKS):
-            if r + CHUNKS_AHEAD < CHUNKS:
+        for r in range(-1, CHUNKS):
+            if 0 <= r and r + CHUNKS_AHEAD < CHUNKS:
                 chunks[r + CHUNKS_AHEAD] = load(r + CHUNKS_AHEAD)
             old = chunks.get(r)
             new = chunks.get(r + 1)
-            far = chunks.get(r + 2)
 
             if new is not None:
                 tanh_of_y(new)
                 tanh_of_half_y(new)
                 square(new, 0, 1.0)
                 square(new, 3, 0.5)
-                cosine(new)
                 if "x" in new:
-                    group_x(new, X_VECTOR_COLS, IN_F - X_VECTOR_COLS, nc.scalar.copy)
+                    new["x_grouped"] = xg_pool.tile(
+                        [P, IN_F, PACK], BF16, align_bytes=64, name="x_grouped"
+                    )
+                    group_x(new, X_VECTOR_COLS, IN_F, nc.scalar.copy)
 
             if old is not None:
                 if r % PASSES == 0:
@@ -250,27 +247,25 @@ def tile_vdl_v_kernel(tc, x, w, b, y, grad_out, out):
                 old["scales"] = dy_pool.tile([P, KINDS, M], U8, align_bytes=64, name="dy_scales")
 
             if old is not None:
-                if "x" in old:
-                    quantise_x(old, r, X_VECTOR_COLS, IN_F - X_VECTOR_COLS)
                 times_grad_relu(old, 2)
-                if "x" in old:
-                    quantise_x(old, r, 0, X_VECTOR_COLS)
-            if far is not None:
-                turns(far, 1)
-            if old is not None:
                 times_grad_tanh(old, 0, 1.0)
-                multiply(old, r, 2, acc)
-            if far is not None:
-                whole_turns(far)
-            if old is not None:
                 times_grad_tanh(old, 3, 0.5)
-                multiply(old, r, 0, acc)
-            if far is not None:
-                part_of_a_turn(far)
+                if "x" in old:
+                    quantise_x(old, r, 1)
+            if new is not None:
+                turns(new, 1)
             if old is not None:
+                if "x" in old:
+                    quantise_x(old, r, 0)
+                multiply(old, r, 2, acc)
+            if new is not None:
+                whole_turns(new)
+            if old is not None:
+                multiply(old, r, 0, acc)
                 times_grad_cos(old, 1)
                 multiply(old, r, 3, acc)
             if new is not None:
+                cosine(new)
                 group_g(new)
             if old is not None:
                 multiply(old, r, LAST_KIND, acc)

@@ -69,6 +69,7 @@ def tile_vdl_v_kernel(tc, x, w, b, y, grad_out, out):
             tiles = {
                 "y": y_sb[:].rearrange("p j (m kind) -> p kind m j", kind=KINDS),
                 "y23": y_sb[:].rearrange("p j (m pair e) -> p pair m j e", pair=2, e=2)[:, 1],
+                "y01": y_sb[:].rearrange("p j (m pair e) -> p pair m j e", pair=2, e=2)[:, 0],
                 "g_raw": g_sb,
             }
             if h == 0:
@@ -80,7 +81,9 @@ def tile_vdl_v_kernel(tc, x, w, b, y, grad_out, out):
 
         def tanh_of_y(tiles):
             th = work.tile([P, M, PACK], F32, name="th0")
-            nc.scalar.activation(out=th[:], in_=tiles["y"][:, 0], func=ACT.Tanh)
+            nc.scalar.activation(
+                out=th[:], in_=tiles["t0"], func=ACT.Tanh, scale=2.0 * math.pi, bias=-0.5 * math.pi
+            )
             tiles["th", 0] = th[:]
 
         def tanh_of_half_y(tiles):
@@ -96,23 +99,24 @@ def tile_vdl_v_kernel(tc, x, w, b, y, grad_out, out):
             nc.scalar.activation(out=sq[:], in_=tiles["th", kind], func=ACT.Square, scale=s)
             tiles["sq", kind] = sq
 
-        def turns(tiles, kind):
-            t = work.tile([P, M, PACK], F32, name="turns")
+        def turns(tiles):
+            t = work.tile([P, 2, M, PACK], F32, name="turns")
             nc.vector.tensor_scalar(
-                out=t[:],
-                in0=tiles["y"][:, kind],
+                out=t[:].rearrange("p e m j -> p m j e"),
+                in0=tiles["y01"],
                 scalar1=1.0 / (2.0 * math.pi),
                 scalar2=0.25,
                 op0=ALU.mult,
                 op1=ALU.add,
             )
-            tiles["turns"] = t
+            tiles["t0"] = t[:, 0]
+            tiles["turns"] = t[:, 1]
 
         def whole_turns(tiles):
             whole = work.tile([P, M, PACK], F32)
             nc.vector.tensor_scalar(
                 out=whole[:],
-                in0=tiles["turns"][:],
+                in0=tiles["turns"],
                 scalar1=ROUND_MAGIC,
                 scalar2=ROUND_MAGIC,
                 op0=ALU.add,
@@ -124,7 +128,7 @@ def tile_vdl_v_kernel(tc, x, w, b, y, grad_out, out):
             frac = work.tile([P, M, PACK], F32)
             cos_y = ready.tile([P, M, PACK], F32)
             nc.vector.tensor_tensor(
-                out=frac[:], in0=tiles["turns"][:], in1=tiles["whole"][:], op=ALU.subtract
+                out=frac[:], in0=tiles["turns"], in1=tiles["whole"][:], op=ALU.subtract
             )
             nc.scalar.activation(out=cos_y[:], in_=frac[:], func=ACT.Sin, scale=2.0 * math.pi)
             tiles["cos"] = cos_y
@@ -223,10 +227,11 @@ def tile_vdl_v_kernel(tc, x, w, b, y, grad_out, out):
             new = chunks.get(r + 1)
 
             if new is not None:
-                tanh_of_y(new)
+                turns(new)
                 tanh_of_half_y(new)
-                square(new, 0, 1.0)
                 square(new, 3, 0.5)
+                tanh_of_y(new)
+                square(new, 0, 1.0)
                 if "x" in new:
                     new["x_grouped"] = xg_pool.tile(
                         [P, IN_F, PACK], BF16, align_bytes=64, name="x_grouped"
@@ -252,8 +257,6 @@ def tile_vdl_v_kernel(tc, x, w, b, y, grad_out, out):
                 times_grad_tanh(old, 3, 0.5)
                 if "x" in old:
                     quantise_x(old, r, 1)
-            if new is not None:
-                turns(new, 1)
             if old is not None:
                 if "x" in old:
                     quantise_x(old, r, 0)

@@ -24,18 +24,65 @@ HALVES = 2
 HALF = OUT_F // HALVES
 M = HALF // KINDS
 assert M == P
+E = M * PACK
 CHUNKS = HALVES * PASSES
 CHUNKS_AHEAD = 4
 
 X_VECTOR_COLS = 384
+YG_BUFS = 4
+DY_BUFS = 4
+X_BUFS = 3
 
-SIGN = (-1.0, 1.0, 1.0, -1.0)
-LAST_KIND = 1
+PAIRS = ((2, 3), (0, 1))
+SIGN = (-1.0, 1.0, 1.0, -0.25)
 
 ROUND_MAGIC = 12582912.0
 
 FLOPS = 2 * TOKENS * IN_F * OUT_F
 BYTES = 2 * TOKENS * IN_F + (4 + 2) * TOKENS * OUT_F + 4 * OUT_F * IN_F
+
+
+A, B = (2, 3), (0, 1)
+
+
+def group_of(i, kind):
+    if kind in A:
+        return A
+    return B if i < PASSES else (kind,)
+
+
+def program():
+    V, S, T, L = [], [], [], []
+    for i in range(CHUNKS):
+        L += [("load", i)] + ([("loadx", i)] if i < PASSES else [])
+    T += [("mm", i, group) for i in range(PASSES) for group in (A, B)]
+    T += [("mm", i, group) for group in (A, (0,), (1,)) for i in range(PASSES, CHUNKS)]
+    V += [("turns", 0), ("whole", 0), ("frac", 0), ("gg", 0)]
+    for c in range(PASSES):
+        V += [("stt", c, 2), ("stt", c, 3), ("stt", c, 0), ("gx", c), ("stt", c, 1), ("q", c, A), ("q", c, B)]
+        V += [("turns", c + 1), ("qx", c, 1), ("whole", c + 1), ("qx", c, 0), ("frac", c + 1), ("gg", c + 1)]
+    for i in range(PASSES, CHUNKS):
+        V += [("stt", i, 2), ("stt", i, 3)]
+        if i + 1 < CHUNKS:
+            V += [("turns", i + 1), ("q", i, A), ("whole", i + 1), ("gg", i + 1), ("frac", i + 1)]
+        else:
+            V += [("stt", PASSES, 0), ("q", i, A)]
+    rest = [(i, kind) for kind in B for i in range(PASSES, CHUNKS)]
+    for k in range(1, len(rest)):
+        V += [("stt", rest[k][0], rest[k][1]), ("q", rest[k - 1][0], (rest[k - 1][1],))]
+    V += [("q", CHUNKS - 1, (1,)), ("out", 1, 1, 1, True)]
+    for i in range(PASSES + 1):
+        S += [("th23", i), ("th0", i), ("sq3", i), ("sq0", i), ("cos", i)]
+        if i < PASSES:
+            S += [("sx", i)]
+    S += [("th23", 5), ("out", 0, 2, 0, False), ("sq3", 5)]
+    S += [("out", 0, 2, 1, False), ("out", 0, 3, 0, False), ("out", 0, 3, 1, False)]
+    S += [("th23", 6), ("th0", 5), ("sq3", 6), ("sq0", 5), ("cos", 5), ("out", 0, 0, 0, False), ("out", 0, 0, 1, False)]
+    S += [("th23", 7), ("th0", 6), ("sq3", 7), ("sq0", 6), ("th0", 7), ("cos", 6), ("sq0", 7), ("cos", 7)]
+    S += [("out", 0, 1, 0, False), ("out", 0, 1, 1, False), ("out", 1, 2, 0, False)]
+    S += [("out", 1, 2, 1, False), ("out", 1, 3, 0, False), ("out", 1, 3, 1, False)]
+    S += [("out", 1, 0, 0, False), ("out", 1, 0, 1, False), ("out", 1, 1, 0, False)]
+    return [L, S, V, T]
 
 
 def tile_vdl_v_kernel(tc, x, w, b, y, grad_out, out):
@@ -48,13 +95,14 @@ def tile_vdl_v_kernel(tc, x, w, b, y, grad_out, out):
 
     with ExitStack() as ctx:
         keep = ctx.enter_context(tc.tile_pool(name="keep", bufs=1))
-        x_pool = ctx.enter_context(tc.tile_pool(name="x_in", bufs=PASSES))
+        x_pool = ctx.enter_context(tc.tile_pool(name="x_in", bufs=X_BUFS))
         xg_pool = ctx.enter_context(tc.tile_pool(name="x_grouped", bufs=2))
-        yg_pool = ctx.enter_context(tc.tile_pool(name="y_g_in", bufs=CHUNKS_AHEAD + 1))
+        yg_pool = ctx.enter_context(tc.tile_pool(name="y_g_in", bufs=YG_BUFS))
         work = ctx.enter_context(tc.tile_pool(name="work", bufs=2))
         ready = ctx.enter_context(tc.tile_pool(name="ready", bufs=3))
-        dy_pool = ctx.enter_context(tc.tile_pool(name="dy", bufs=3))
-        stage = ctx.enter_context(tc.tile_pool(name="stage", bufs=KINDS * N_TILES))
+        late = ctx.enter_context(tc.tile_pool(name="late", bufs=PASSES + 2))
+        dy_pool = ctx.enter_context(tc.tile_pool(name="dy", bufs=DY_BUFS))
+        stage = ctx.enter_context(tc.tile_pool(name="stage", bufs=6))
         psum = ctx.enter_context(tc.psum_pool(name="acc", bufs=1))
         ctx.enter_context(tc.manual_schedule())
 
@@ -63,152 +111,161 @@ def tile_vdl_v_kernel(tc, x, w, b, y, grad_out, out):
 
         def load(i):
             h, c = divmod(i, PASSES)
-            y_sb = yg_pool.tile([P, PACK, HALF], F32)
-            g_sb = yg_pool.tile([P, PACK * HALF], BF16)
+            y_sb = yg_pool.tile([P, PACK, HALF], F32, name="y_sb")
+            g_sb = yg_pool.tile([P, PACK * HALF], BF16, name="g_sb")
             nc.sync.dma_start(out=y_sb[:], in_=y_rows[h, c])
-            tiles = {
-                "y": y_sb[:].rearrange("p j (m kind) -> p kind m j", kind=KINDS),
-                "y23": y_sb[:].rearrange("p j (m pair e) -> p pair m j e", pair=2, e=2)[:, 1],
-                "y01": y_sb[:].rearrange("p j (m pair e) -> p pair m j e", pair=2, e=2)[:, 0],
-                "g_raw": g_sb,
-            }
-            if h == 0:
-                x_raw = x_pool.tile([P, PACK, IN_F], BF16)
-                nc.sync.dma_start(out=x_raw[:], in_=x_rows[c])
-                tiles["x"] = x_raw
             nc.sync.dma_start(out=g_sb[:].rearrange("p (j o) -> p j o", j=PACK), in_=g_rows[h, c])
-            return tiles
+            by_pair = y_sb[:].rearrange("p j (m pair e) -> p pair m j e", pair=2, e=2)
+            return {"y01": by_pair[:, 0], "y23": by_pair[:, 1], "g_raw": g_sb}
 
-        def tanh_of_y(tiles):
-            th = work.tile([P, M, PACK], F32, name="th0")
-            nc.scalar.activation(
-                out=th[:], in_=tiles["t0"], func=ACT.Tanh, scale=2.0 * math.pi, bias=-0.5 * math.pi
-            )
-            tiles["th", 0] = th[:]
+        def load_x(t, c):
+            x_raw = x_pool.tile([P, PACK, IN_F], BF16, name="x_raw")
+            nc.sync.dma_start(out=x_raw[:], in_=x_rows[c])
+            t["x"] = x_raw
 
-        def tanh_of_half_y(tiles):
-            th = ready.tile([P, 2, M, PACK], F32, name="th23")
-            nc.scalar.activation(
-                out=th[:].rearrange("p e m j -> p m j e"), in_=tiles["y23"], func=ACT.Tanh, scale=0.5
-            )
-            tiles["th", 2] = th[:, 0]
-            tiles["th", 3] = th[:, 1]
+        def pairwise(tile):
+            return tile[:].rearrange("p e (m j) -> p m j e", j=PACK)
 
-        def square(tiles, kind, s):
-            sq = ready.tile([P, M, PACK], F32, name="sq", tag="sq%d" % kind)
-            nc.scalar.activation(out=sq[:], in_=tiles["th", kind], func=ACT.Square, scale=s)
-            tiles["sq", kind] = sq
+        def scalar_23(t):
+            th = ready.tile([P, 2, E], F32, name="th23")
+            sq = ready.tile([P, E], F32, name="sq3")
+            nc.scalar.activation(out=pairwise(th), in_=t["y23"], func=ACT.Tanh, scale=0.5)
+            t["th2"] = th[:, 0]
+            t["th3"] = th[:, 1]
+            t["sq3"] = sq
 
-        def turns(tiles):
-            t = work.tile([P, 2, M, PACK], F32, name="turns")
+        def scalar_sq3(t):
+            nc.scalar.activation(out=t["sq3"][:], in_=t["th3"], func=ACT.Square)
+
+        def turns(t, on_scalar):
+            tt = ready.tile([P, 2, E], F32, name="turns")
+            if on_scalar:
+                nc.scalar.activation(
+                    out=pairwise(tt), in_=t["y01"], func=ACT.Identity, scale=1.0 / (2.0 * math.pi), bias=0.25
+                )
+            else:
+                nc.vector.tensor_scalar(
+                    out=pairwise(tt), in0=t["y01"], scalar1=1.0 / (2.0 * math.pi), scalar2=0.25,
+                    op0=ALU.mult, op1=ALU.add,
+                )
+            t["t0"] = tt[:, 0]
+            t["t1"] = tt[:, 1]
+
+        def whole_turns(t):
+            whole = work.tile([P, E], F32, name="whole")
             nc.vector.tensor_scalar(
-                out=t[:].rearrange("p e m j -> p m j e"),
-                in0=tiles["y01"],
-                scalar1=1.0 / (2.0 * math.pi),
-                scalar2=0.25,
-                op0=ALU.mult,
-                op1=ALU.add,
+                out=whole[:], in0=t["t1"], scalar1=ROUND_MAGIC, scalar2=ROUND_MAGIC,
+                op0=ALU.add, op1=ALU.subtract,
             )
-            tiles["t0"] = t[:, 0]
-            tiles["turns"] = t[:, 1]
+            t["whole"] = whole
 
-        def whole_turns(tiles):
-            whole = work.tile([P, M, PACK], F32)
-            nc.vector.tensor_scalar(
-                out=whole[:],
-                in0=tiles["turns"],
-                scalar1=ROUND_MAGIC,
-                scalar2=ROUND_MAGIC,
-                op0=ALU.add,
-                op1=ALU.subtract,
+        def fraction(t):
+            frac = ready.tile([P, E], F32, name="frac")
+            nc.vector.tensor_tensor(out=frac[:], in0=t["t1"], in1=t["whole"][:], op=ALU.subtract)
+            t["frac"] = frac
+
+        def scalar_tanh0(t):
+            th = work.tile([P, E], F32, name="th0")
+            nc.scalar.activation(
+                out=th[:], in_=t["t0"], func=ACT.Tanh, scale=2.0 * math.pi, bias=-0.5 * math.pi
             )
-            tiles["whole"] = whole
+            t["th0"] = th
 
-        def cosine(tiles):
-            frac = work.tile([P, M, PACK], F32)
-            cos_y = ready.tile([P, M, PACK], F32)
-            nc.vector.tensor_tensor(
-                out=frac[:], in0=tiles["turns"], in1=tiles["whole"][:], op=ALU.subtract
-            )
-            nc.scalar.activation(out=cos_y[:], in_=frac[:], func=ACT.Sin, scale=2.0 * math.pi)
-            tiles["cos"] = cos_y
+        def scalar_sq0(t):
+            sq = late.tile([P, E], F32, name="sq0")
+            nc.scalar.activation(out=sq[:], in_=t["th0"][:], func=ACT.Square)
+            t["sq0"] = sq
 
-        def group_g(tiles):
-            words = ready.tile([P, PACK * HALF], BF16, name="g_words")
+        def scalar_cos(t):
+            cos_y = late.tile([P, E], F32, name="cos_y")
+            nc.scalar.activation(out=cos_y[:], in_=t["frac"][:], func=ACT.Sin, scale=2.0 * math.pi)
+            t["cos"] = cos_y
+
+        def group_g(t):
+            words = late.tile([P, KINDS * E], BF16, name="g_words")
             nc.vector.tensor_copy(
-                out=words[:].bitcast(F32).rearrange("p (pair j) -> p pair j", j=PACK),
-                in_=tiles["g_raw"][:].bitcast(F32).rearrange("p (j pair) -> p pair j", j=PACK),
+                out=words[:].bitcast(F32).rearrange("p (hi m j) -> p m hi j", hi=2, j=PACK),
+                in_=t["g_raw"][:].bitcast(F32).rearrange("p (j m hi) -> p m hi j", j=PACK, hi=2),
             )
-            by_kind = words[:].rearrange("p (m hi j lo) -> p hi lo m j", hi=2, j=PACK, lo=2)
             for kind in range(KINDS):
-                tiles["g", kind] = by_kind[:, kind // 2, kind % 2]
+                first = (kind // 2) * 2 * E + kind % 2
+                t["g", kind] = words[:, first : first + 2 * E - 1 : 2]
 
-        def group_x(tiles, first, last, copy):
+        def group_x(t, first, last, copy):
             copy(
-                out=tiles["x_grouped"][:, first:last, :].rearrange("p (r i) j -> p r j i", i=4),
-                in_=tiles["x"][:, :, first:last].rearrange("p j (r i) -> p r j i", i=4),
+                out=t["x_grouped"][:, first:last, :].rearrange("p (r i) j -> p r j i", i=4),
+                in_=t["x"][:, :, first:last].rearrange("p j (r i) -> p r j i", i=4),
             )
 
-        def quantise_x(tiles, c, n):
+        def scalar_x(t):
+            t["x_grouped"] = xg_pool.tile([P, IN_F, PACK], BF16, align_bytes=64, name="x_grouped")
+            group_x(t, X_VECTOR_COLS, IN_F, nc.scalar.copy)
+
+        def vector_x(t):
+            group_x(t, 0, X_VECTOR_COLS, nc.vector.tensor_copy)
+
+        def quantise_x(t, c, n):
             n_cols = slice(n * N_TILE, (n + 1) * N_TILE)
             nc.vector.quantize_mx(
                 out=x_codes[:, c, n_cols].bitcast(E4M3X4),
                 scales=x_scales[:, c, n_cols],
-                in_=tiles["x_grouped"][:, n_cols, :].rearrange("p col j -> p (col j)"),
+                in_=t["x_grouped"][:, n_cols, :].rearrange("p col j -> p (col j)"),
             )
 
-        def times_grad_relu(tiles, kind):
-            nc.vector.scalar_tensor_tensor(
-                out=tiles["dy"][:, kind],
-                in0=tiles["th", kind],
-                scalar=0.0,
-                in1=tiles["g", kind],
-                op0=ALU.is_gt,
-                op1=ALU.mult,
-            )
-
-        def times_grad_tanh(tiles, kind, s):
-            nc.vector.scalar_tensor_tensor(
-                out=tiles["dy"][:, kind],
-                in0=tiles["sq", kind][:],
-                scalar=s * s,
-                in1=tiles["g", kind],
-                op0=ALU.subtract,
-                op1=ALU.mult,
-            )
-
-        def times_grad_cos(tiles, kind):
-            nc.vector.tensor_tensor(
-                out=tiles["dy"][:, kind], in0=tiles["cos"][:], in1=tiles["g", kind], op=ALU.mult
-            )
-
-        def multiply(tiles, i, kind, acc):
-            h, c = divmod(i, PASSES)
-            nc.vector.quantize_mx(
-                out=tiles["codes"][:, kind].bitcast(E5M2X4),
-                scales=tiles["scales"][:, kind],
-                in_=tiles["dy"][:, kind].rearrange("p m j -> p (m j)"),
-            )
-            for n in range(N_TILES):
-                n_cols = slice(n * N_TILE, (n + 1) * N_TILE)
-                nc.tensor.matmul_mx(
-                    out=acc[kind][n][:],
-                    lhsT=tiles["codes"][:, kind].bitcast(E5M2X4),
-                    lhsT_scale=tiles["scales"][:, kind],
-                    rhs=x_codes[:, c, n_cols].bitcast(E4M3X4),
-                    rhs_scale=x_scales[:, c, n_cols],
-                    start=(c == 0),
-                    stop=(c == PASSES - 1),
+        def times_grad(t, kind, group):
+            s = group.index(kind)
+            if ("dy", group) not in t:
+                t["dy", group] = dy_pool.tile([P, len(group), E], BF16, align_bytes=64, name="dy")
+            dy = t["dy", group]
+            if kind == 2:
+                nc.vector.scalar_tensor_tensor(
+                    out=dy[:, s], in0=t["th2"], scalar=0.0, in1=t["g", 2], op0=ALU.is_gt, op1=ALU.mult
                 )
-                if c == PASSES - 1:
-                    result = stage.tile([P, N_TILE], F32)
-                    if i == CHUNKS - 1 and kind == LAST_KIND and n == N_TILES - 1:
-                        nc.vector.tensor_scalar_mul(
-                            out=result[:], in0=acc[kind][n][:], scalar1=SIGN[kind]
-                        )
-                    else:
-                        nc.scalar.mul(out=result[:], in_=acc[kind][n][:], mul=SIGN[kind])
-                    nc.sync.dma_start(out=out_rows[h, kind][:, n_cols], in_=result[:])
+            elif kind == 1:
+                nc.vector.tensor_tensor(out=dy[:, s], in0=t["cos"][:], in1=t["g", 1], op=ALU.mult)
+            else:
+                nc.vector.scalar_tensor_tensor(
+                    out=dy[:, s], in0=t["sq%d" % kind][:], scalar=1.0, in1=t["g", kind],
+                    op0=ALU.subtract, op1=ALU.mult,
+                )
+
+        def quantise_dy(t, pair):
+            codes = dy_pool.tile([P, len(pair), M], U32, align_bytes=64, name="dy_codes")
+            scales = dy_pool.tile([P, len(pair), M], U8, align_bytes=64, name="dy_scales")
+            nc.vector.quantize_mx(
+                out=codes[:].rearrange("p s m -> p (s m)").bitcast(E5M2X4),
+                scales=scales[:].rearrange("p s m -> p (s m)"),
+                in_=t["dy", pair][:].rearrange("p s e -> p (s e)"),
+            )
+            t["codes", pair] = codes
+            t["scales", pair] = scales
+
+        acc = {}
+
+        def products(t, i, pair):
+            h, c = divmod(i, PASSES)
+            for s, kind in enumerate(pair):
+                for n in range(N_TILES):
+                    if c == 0:
+                        acc[kind, n] = psum.tile([P, N_TILE], F32, name="acc%d%d" % (kind, n))
+                    n_cols = slice(n * N_TILE, (n + 1) * N_TILE)
+                    nc.tensor.matmul_mx(
+                        out=acc[kind, n][:],
+                        lhsT=t["codes", pair][:, s].bitcast(E5M2X4),
+                        lhsT_scale=t["scales", pair][:, s],
+                        rhs=x_codes[:, c, n_cols].bitcast(E4M3X4),
+                        rhs_scale=x_scales[:, c, n_cols],
+                        start=(c == 0),
+                        stop=(c == PASSES - 1),
+                    )
+
+        def send_out(h, kind, n, by_vector):
+            result = stage.tile([P, N_TILE], F32, name="result")
+            if by_vector:
+                nc.vector.tensor_scalar_mul(out=result[:], in0=acc[kind, n][:], scalar1=SIGN[kind])
+            else:
+                nc.scalar.mul(out=result[:], in_=acc[kind, n][:], mul=SIGN[kind])
+            nc.sync.dma_start(out=out_rows[h, kind][:, n * N_TILE : (n + 1) * N_TILE], in_=result[:])
 
         zero = keep.tile([P, 1], F32)
         unused = keep.tile([P, 1], F32)
@@ -216,61 +273,88 @@ def tile_vdl_v_kernel(tc, x, w, b, y, grad_out, out):
         nc.scalar.activation(out=unused[:], in_=zero[:], func=ACT.Silu)
 
         chunks = {}
-        for i in range(CHUNKS_AHEAD):
-            chunks[i] = load(i)
 
-        acc = None
-        for r in range(-1, CHUNKS):
-            if 0 <= r and r + CHUNKS_AHEAD < CHUNKS:
-                chunks[r + CHUNKS_AHEAD] = load(r + CHUNKS_AHEAD)
-            old = chunks.get(r)
-            new = chunks.get(r + 1)
+        def run(step):
+            name, i = step[0], step[1]
+            if name == "load":
+                chunks[i] = load(i)
+                return
+            if name == "out":
+                send_out(i, step[2], step[3], step[4])
+                return
+            t = chunks[i]
+            if name == "loadx": load_x(t, i)
+            elif name == "th23": scalar_23(t)
+            elif name == "sq3": scalar_sq3(t)
+            elif name == "th0": scalar_tanh0(t)
+            elif name == "sq0": scalar_sq0(t)
+            elif name == "cos": scalar_cos(t)
+            elif name == "sx": scalar_x(t)
+            elif name == "turns": turns(t, False)
+            elif name == "whole": whole_turns(t)
+            elif name == "frac": fraction(t)
+            elif name == "gg": group_g(t)
+            elif name == "gx": vector_x(t)
+            elif name == "qx": quantise_x(t, i, step[2])
+            elif name == "stt": times_grad(t, step[2], group_of(i, step[2]))
+            elif name == "q": quantise_dy(t, step[2])
+            elif name == "mm": products(t, i, step[2])
+            else: assert False, name
 
-            if new is not None:
-                turns(new)
-                tanh_of_half_y(new)
-                square(new, 3, 0.5)
-                tanh_of_y(new)
-                square(new, 0, 1.0)
-                if "x" in new:
-                    new["x_grouped"] = xg_pool.tile(
-                        [P, IN_F, PACK], BF16, align_bytes=64, name="x_grouped"
-                    )
-                    group_x(new, X_VECTOR_COLS, IN_F, nc.scalar.copy)
+        def needs(step):
+            name, i = step[0], step[1]
+            if name == "load":
+                k = i - YG_BUFS
+                return [("th23", k), ("turns", k), ("gg", k)] if k >= 0 else []
+            if name == "loadx":
+                k = i - X_BUFS
+                return [("load", i)] + ([("sx", k), ("gx", k)] if k >= 0 else [])
+            if name == "out":
+                return [("mm", i * PASSES + PASSES - 1, group_of(i * PASSES, step[2]))]
+            if name == "mm":
+                h, c = divmod(i, PASSES)
+                req = [("q", i, step[2]), ("qx", c, 0), ("qx", c, 1)]
+                if h == 1 and c == 0:
+                    req += [("out", 0, kind, n) for kind in step[2] for n in range(N_TILES)]
+                return req
+            table = {
+                "th23": ["load"], "turns": ["load"], "gg": ["load"], "sx": ["loadx"], "gx": ["sx"],
+                "sq3": ["th23"], "th0": ["turns"], "sq0": ["th0"], "whole": ["turns"], "frac": ["whole"],
+                "cos": ["frac"],
+            }
+            turn = {
+                "th23": (3, [("sq3",), ("stt", 2), ("stt", 3)]), "turns": (3, [("th0",), ("frac",)]),
+                "whole": (2, [("frac",)]), "frac": (3, [("cos",)]), "th0": (2, [("sq0",)]),
+                "sq0": (PASSES + 2, [("stt", 0)]), "cos": (PASSES + 2, [("stt", 1)]),
+                "gg": (PASSES + 2, [("stt", 0), ("stt", 1), ("stt", 2), ("stt", 3)]),
+                "sx": (2, [("qx", 0), ("qx", 1)]),
+            }
+            old = []
+            if name in turn and i - turn[name][0] >= 0:
+                old = [(r[0], i - turn[name][0]) + r[1:] for r in turn[name][1]]
+            if name in table:
+                return old + [(a, i) for a in table[name]]
+            if name == "qx":
+                return [("gx", i), ("sx", i)]
+            if name == "stt":
+                return [(("th23", "cos", "th23", "sq3")[step[2]] if step[2] else "sq0", i), ("gg", i)]
+            if name == "q":
+                k = queues[3].index(("mm", i, step[2])) - DY_BUFS
+                return [("stt", i, kind) for kind in step[2]] + ([queues[3][k]] if k >= 0 else [])
+            assert False, name
 
-            if old is not None:
-                if r % PASSES == 0:
-                    acc = [
-                        [
-                            psum.tile([P, N_TILE], F32, name="acc%d%d" % (kind, n))
-                            for n in range(N_TILES)
-                        ]
-                        for kind in range(KINDS)
-                    ]
-                old["dy"] = dy_pool.tile([P, KINDS, M, PACK], BF16, align_bytes=64, name="dy")
-                old["codes"] = dy_pool.tile([P, KINDS, M], U32, align_bytes=64, name="dy_codes")
-                old["scales"] = dy_pool.tile([P, KINDS, M], U8, align_bytes=64, name="dy_scales")
-
-            if old is not None:
-                times_grad_relu(old, 2)
-                times_grad_tanh(old, 0, 1.0)
-                times_grad_tanh(old, 3, 0.5)
-                if "x" in old:
-                    quantise_x(old, r, 1)
-            if old is not None:
-                if "x" in old:
-                    quantise_x(old, r, 0)
-                multiply(old, r, 2, acc)
-            if new is not None:
-                whole_turns(new)
-            if old is not None:
-                multiply(old, r, 0, acc)
-                times_grad_cos(old, 1)
-                multiply(old, r, 3, acc)
-            if new is not None:
-                cosine(new)
-                group_g(new)
-            if old is not None:
-                multiply(old, r, LAST_KIND, acc)
-            if new is not None and "x" in new:
-                group_x(new, 0, X_VECTOR_COLS, nc.vector.tensor_copy)
+        queues = program()
+        at = [0 for q in queues]
+        done = set()
+        left = sum(len(q) for q in queues)
+        while left:
+            moved = False
+            for k, q in enumerate(queues):
+                while at[k] < len(q) and all(r in done for r in needs(q[at[k]])):
+                    step = q[at[k]]
+                    run(step)
+                    done.add(step[:4] if step[0] == "out" else step)
+                    at[k] += 1
+                    left -= 1
+                    moved = True
+            assert moved, [q[at[k]] for k, q in enumerate(queues) if at[k] < len(q)]

@@ -60,7 +60,7 @@ def program():
     V += [("turns", 0), ("whole", 0), ("frac", 0), ("gg", 0)]
     for c in range(PASSES):
         V += [("stt", c, 2), ("stt", c, 3), ("stt", c, 0), ("gx", c), ("stt", c, 1), ("q", c, A), ("q", c, B)]
-        V += [("turns", c + 1), ("qx", c, 1), ("whole", c + 1), ("qx", c, 0), ("frac", c + 1), ("gg", c + 1)]
+        V += [("turns", c + 1), ("qx", c, 1), ("whole", c + 1), ("gg", c + 1), ("qx", c, 0), ("frac", c + 1)]
     for i in range(PASSES, CHUNKS):
         V += [("stt", i, 2), ("stt", i, 3)]
         if i + 1 < CHUNKS:

@@ -2,6 +2,7 @@ import math
 from contextlib import ExitStack
 
 import concourse.mybir as mybir
+from concourse.masks import make_identity
 
 F32 = mybir.dt.float32
 BF16 = mybir.dt.bfloat16
@@ -48,19 +49,23 @@ A, B = (2, 3), (0, 1)
 def group_of(i, kind):
     if kind in A:
         return A
-    return B if i < PASSES else (kind,)
+    return (kind,)
 
 
 def program():
     V, S, T, L = [], [], [], []
     for i in range(CHUNKS):
         L += [("load", i)] + ([("loadx", i)] if i < PASSES else [])
-    T += [("mm", i, group) for i in range(PASSES) for group in (A, B)]
-    T += [("mm", i, group) for group in (A, (0,), (1,)) for i in range(PASSES, CHUNKS)]
-    V += [("turns", 0), ("whole", 0), ("frac", 0), ("gg", 0)]
+    T += [("stage", 0)]
     for c in range(PASSES):
-        V += [("stt", c, 2), ("stt", c, 3), ("stt", c, 0), ("gx", c), ("stt", c, 1), ("q", c, A), ("q", c, B)]
-        V += [("turns", c + 1), ("qx", c, 1), ("whole", c + 1), ("gg", c + 1), ("qx", c, 0), ("frac", c + 1)]
+        T += ([("stage", c + 1)] if c + 1 < PASSES else []) + [("mm", c, A), ("mm", c, (0,))]
+    T += [("mm", c, (1,)) for c in range(PASSES)]
+    T += [("mm", i, group) for group in (A, (0,), (1,)) for i in range(PASSES, CHUNKS)]
+    V += [("turns", 0), ("whole", 0), ("frac", 0)]
+    for c in range(PASSES):
+        V += [("stt", c, 2), ("stt", c, 3), ("stt", c, 0), ("gx", c), ("stt", c, 1), ("q", c, A), ("q", c, (0,))]
+        V += [("turns", c + 1), ("q", c, (1,)), ("qx", c, 1), ("whole", c + 1)]
+        V += ([("gg", c + 1)] if c + 1 == PASSES else []) + [("qx", c, 0), ("frac", c + 1)]
     for i in range(PASSES, CHUNKS):
         V += [("stt", i, 2), ("stt", i, 3)]
         if i + 1 < CHUNKS:
@@ -108,6 +113,8 @@ def tile_vdl_v_kernel(tc, x, w, b, y, grad_out, out):
 
         x_codes = keep.tile([P, PASSES, IN_F], U32, align_bytes=64)
         x_scales = keep.tile([P, PASSES, IN_F], U8, align_bytes=64)
+        ident = keep.tile([P, P], BF16)
+        make_identity(nc, ident[:])
 
         def load(i):
             h, c = divmod(i, PASSES)
@@ -229,9 +236,23 @@ def tile_vdl_v_kernel(tc, x, w, b, y, grad_out, out):
                     op0=ALU.subtract, op1=ALU.mult,
                 )
 
-        def quantise_dy(t, pair):
-            codes = dy_pool.tile([P, len(pair), M], U32, align_bytes=64, name="dy_codes")
-            scales = dy_pool.tile([P, len(pair), M], U8, align_bytes=64, name="dy_scales")
+        def stage_g(t):
+            for b, pair in enumerate((A, B)):
+                bank = psum.tile([P, 2, E], BF16, name="acc1%d" % b)
+                for s, kind in enumerate(pair):
+                    nc.tensor.matmul(
+                        out=bank[:, s].rearrange("p (m j) -> p m j", j=PACK),
+                        lhsT=ident[:],
+                        rhs=t["g_raw"][:].rearrange("p (j m k) -> p k m j", j=PACK, k=KINDS)[:, kind],
+                        start=True,
+                        stop=True,
+                    )
+                    t["g", kind] = bank[:, s]
+
+        def quantise_dy(t, pair, kept):
+            pool = late if kept else dy_pool
+            codes = pool.tile([P, len(pair), M], U32, align_bytes=64, name="dy_codes")
+            scales = pool.tile([P, len(pair), M], U8, align_bytes=64, name="dy_scales")
             nc.vector.quantize_mx(
                 out=codes[:].rearrange("p s m -> p (s m)").bitcast(E5M2X4),
                 scales=scales[:].rearrange("p s m -> p (s m)"),
@@ -297,7 +318,8 @@ def tile_vdl_v_kernel(tc, x, w, b, y, grad_out, out):
             elif name == "gx": vector_x(t)
             elif name == "qx": quantise_x(t, i, step[2])
             elif name == "stt": times_grad(t, step[2], group_of(i, step[2]))
-            elif name == "q": quantise_dy(t, step[2])
+            elif name == "q": quantise_dy(t, step[2], i < PASSES and step[2] == (1,))
+            elif name == "stage": stage_g(t)
             elif name == "mm": products(t, i, step[2])
             else: assert False, name
 
@@ -305,7 +327,7 @@ def tile_vdl_v_kernel(tc, x, w, b, y, grad_out, out):
             name, i = step[0], step[1]
             if name == "load":
                 k = i - YG_BUFS
-                return [("th23", k), ("turns", k), ("gg", k)] if k >= 0 else []
+                return [("th23", k), ("turns", k), ("stage" if k < PASSES else "gg", k)] if k >= 0 else []
             if name == "loadx":
                 k = i - X_BUFS
                 return [("load", i)] + ([("sx", k), ("gx", k)] if k >= 0 else [])
@@ -314,6 +336,8 @@ def tile_vdl_v_kernel(tc, x, w, b, y, grad_out, out):
             if name == "mm":
                 h, c = divmod(i, PASSES)
                 req = [("q", i, step[2]), ("qx", c, 0), ("qx", c, 1)]
+                if i == 0 and step[2] == (1,):
+                    req += [("stt", PASSES - 1, kind) for kind in range(KINDS)]
                 if h == 1 and c == 0:
                     req += [("out", 0, kind, n) for kind in step[2] for n in range(N_TILES)]
                 return req
@@ -336,11 +360,15 @@ def tile_vdl_v_kernel(tc, x, w, b, y, grad_out, out):
                 return old + [(a, i) for a in table[name]]
             if name == "qx":
                 return [("gx", i), ("sx", i)]
+            if name == "stage":
+                return [("load", i)] + ([("stt", i - 1, kind) for kind in range(KINDS)] if i else [])
             if name == "stt":
-                return [(("th23", "cos", "th23", "sq3")[step[2]] if step[2] else "sq0", i), ("gg", i)]
+                made = ("th23", "cos", "th23", "sq3")[step[2]] if step[2] else "sq0"
+                return [(made, i), ("stage" if i < PASSES else "gg", i)]
             if name == "q":
-                k = queues[3].index(("mm", i, step[2])) - DY_BUFS
-                return [("stt", i, kind) for kind in step[2]] + ([queues[3][k]] if k >= 0 else [])
+                mine = [s for s in queues[3] if s[0] == "mm" and not (s[1] < PASSES and s[2] == (1,))]
+                k = mine.index(("mm", i, step[2])) - DY_BUFS if ("mm", i, step[2]) in mine else -1
+                return [("stt", i, kind) for kind in step[2]] + ([mine[k]] if k >= 0 else [])
             assert False, name
 
         queues = program()

@@ -29,7 +29,7 @@ E = M * PACK
 CHUNKS = HALVES * PASSES
 CHUNKS_AHEAD = 4
 
-X_VECTOR_COLS = 384
+X_VECTOR_COLS = 320
 YG_BUFS = 4
 DY_BUFS = 4
 X_BUFS = 3

import math
from contextlib import ExitStack

import concourse.mybir as mybir
from concourse.masks import make_identity

F32 = mybir.dt.float32
BF16 = mybir.dt.bfloat16
U32 = mybir.dt.uint32
U8 = mybir.dt.uint8
E4M3X4 = mybir.dt.float8_e4m3fn_x4
E5M2X4 = mybir.dt.float8_e5m2_x4
ACT = mybir.ActivationFunctionType
ALU = mybir.AluOpType

TOKENS, IN_F, OUT_F, KINDS = 2048, 1024, 1024, 4

P = 128
PACK = 4
K_PASS = P * PACK
PASSES = TOKENS // K_PASS
N_TILE = 512
N_TILES = IN_F // N_TILE
HALVES = 2
HALF = OUT_F // HALVES
M = HALF // KINDS
assert M == P
E = M * PACK
CHUNKS = HALVES * PASSES
CHUNKS_AHEAD = 4

X_VECTOR_COLS = 320
YG_BUFS = 4
DY_BUFS = 4
X_BUFS = 3

PAIRS = ((2, 3), (0, 1))
SIGN = (-1.0, 1.0, 1.0, -0.25)

ROUND_MAGIC = 12582912.0

FLOPS = 2 * TOKENS * IN_F * OUT_F
BYTES = 2 * TOKENS * IN_F + (4 + 2) * TOKENS * OUT_F + 4 * OUT_F * IN_F


A, B = (2, 3), (0, 1)


def group_of(i, kind):
    if kind in A:
        return A
    return (kind,)


def program():
    V, S, T, L = [], [], [], []
    for i in range(CHUNKS):
        L += [("load", i)] + ([("loadx", i)] if i < PASSES else [])
    T += [("stage", 0)]
    for c in range(PASSES):
        T += ([("stage", c + 1)] if c + 1 < PASSES else []) + [("mm", c, A), ("mm", c, (0,))]
    T += [("mm", c, (1,)) for c in range(PASSES)]
    T += [("mm", i, group) for group in (A, (0,), (1,)) for i in range(PASSES, CHUNKS)]
    V += [("turns", 0), ("whole", 0), ("frac", 0)]
    for c in range(PASSES):
        V += [("stt", c, 2), ("stt", c, 3), ("stt", c, 0), ("gx", c), ("stt", c, 1), ("q", c, A), ("q", c, (0,))]
        V += [("turns", c + 1), ("q", c, (1,)), ("qx", c, 1), ("whole", c + 1)]
        V += ([("gg", c + 1)] if c + 1 == PASSES else []) + [("qx", c, 0), ("frac", c + 1)]
    for i in range(PASSES, CHUNKS):
        V += [("stt", i, 2), ("stt", i, 3)]
        if i + 1 < CHUNKS:
            V += [("turns", i + 1), ("q", i, A), ("whole", i + 1), ("gg", i + 1), ("frac", i + 1)]
        else:
            V += [("stt", PASSES, 0), ("q", i, A)]
    rest = [(i, kind) for kind in B for i in range(PASSES, CHUNKS)]
    for k in range(1, len(rest)):
        V += [("stt", rest[k][0], rest[k][1]), ("q", rest[k - 1][0], (rest[k - 1][1],))]
    V += [("q", CHUNKS - 1, (1,)), ("out", 1, 1, 1, True)]
    for i in range(PASSES + 1):
        S += [("th23", i), ("th0", i), ("sq3", i), ("sq0", i), ("cos", i)]
        if i < PASSES:
            S += [("sx", i)]
    S += [("th23", 5), ("out", 0, 2, 0, False), ("sq3", 5)]
    S += [("out", 0, 2, 1, False), ("out", 0, 3, 0, False), ("out", 0, 3, 1, False)]
    S += [("th23", 6), ("th0", 5), ("sq3", 6), ("sq0", 5), ("cos", 5), ("out", 0, 0, 0, False), ("out", 0, 0, 1, False)]
    S += [("th23", 7), ("th0", 6), ("sq3", 7), ("sq0", 6), ("th0", 7), ("cos", 6), ("sq0", 7), ("cos", 7)]
    S += [("out", 0, 1, 0, False), ("out", 0, 1, 1, False), ("out", 1, 2, 0, False)]
    S += [("out", 1, 2, 1, False), ("out", 1, 3, 0, False), ("out", 1, 3, 1, False)]
    S += [("out", 1, 0, 0, False), ("out", 1, 0, 1, False), ("out", 1, 1, 0, False)]
    return [L, S, V, T]


def tile_vdl_v_kernel(tc, x, w, b, y, grad_out, out):
    nc = tc.nc

    x_rows = x.rearrange("(c p j) i -> c p j i", p=P, j=PACK)
    y_rows = y.rearrange("(c p j) (h o) -> h c p j o", p=P, j=PACK, h=HALVES)
    g_rows = grad_out.rearrange("(c p j) (h o) -> h c p j o", p=P, j=PACK, h=HALVES)
    out_rows = out.rearrange("(h m kind) i -> h kind m i", h=HALVES, kind=KINDS)

    with ExitStack() as ctx:
        keep = ctx.enter_context(tc.tile_pool(name="keep", bufs=1))
        x_pool = ctx.enter_context(tc.tile_pool(name="x_in", bufs=X_BUFS))
        xg_pool = ctx.enter_context(tc.tile_pool(name="x_grouped", bufs=2))
        yg_pool = ctx.enter_context(tc.tile_pool(name="y_g_in", bufs=YG_BUFS))
        work = ctx.enter_context(tc.tile_pool(name="work", bufs=2))
        ready = ctx.enter_context(tc.tile_pool(name="ready", bufs=3))
        late = ctx.enter_context(tc.tile_pool(name="late", bufs=PASSES + 2))
        dy_pool = ctx.enter_context(tc.tile_pool(name="dy", bufs=DY_BUFS))
        stage = ctx.enter_context(tc.tile_pool(name="stage", bufs=6))
        psum = ctx.enter_context(tc.psum_pool(name="acc", bufs=1))
        ctx.enter_context(tc.manual_schedule())

        x_codes = keep.tile([P, PASSES, IN_F], U32, align_bytes=64)
        x_scales = keep.tile([P, PASSES, IN_F], U8, align_bytes=64)
        ident = keep.tile([P, P], BF16)
        make_identity(nc, ident[:])

        def load(i):
            h, c = divmod(i, PASSES)
            y_sb = yg_pool.tile([P, PACK, HALF], F32, name="y_sb")
            g_sb = yg_pool.tile([P, PACK * HALF], BF16, name="g_sb")
            nc.sync.dma_start(out=y_sb[:], in_=y_rows[h, c])
            nc.sync.dma_start(out=g_sb[:].rearrange("p (j o) -> p j o", j=PACK), in_=g_rows[h, c])
            by_pair = y_sb[:].rearrange("p j (m pair e) -> p pair m j e", pair=2, e=2)
            return {"y01": by_pair[:, 0], "y23": by_pair[:, 1], "g_raw": g_sb}

        def load_x(t, c):
            x_raw = x_pool.tile([P, PACK, IN_F], BF16, name="x_raw")
            nc.sync.dma_start(out=x_raw[:], in_=x_rows[c])
            t["x"] = x_raw

        def pairwise(tile):
            return tile[:].rearrange("p e (m j) -> p m j e", j=PACK)

        def scalar_23(t):
            th = ready.tile([P, 2, E], F32, name="th23")
            sq = ready.tile([P, E], F32, name="sq3")
            nc.scalar.activation(out=pairwise(th), in_=t["y23"], func=ACT.Tanh, scale=0.5)
            t["th2"] = th[:, 0]
            t["th3"] = th[:, 1]
            t["sq3"] = sq

        def scalar_sq3(t):
            nc.scalar.activation(out=t["sq3"][:], in_=t["th3"], func=ACT.Square)

        def turns(t, on_scalar):
            tt = ready.tile([P, 2, E], F32, name="turns")
            if on_scalar:
                nc.scalar.activation(
                    out=pairwise(tt), in_=t["y01"], func=ACT.Identity, scale=1.0 / (2.0 * math.pi), bias=0.25
                )
            else:
                nc.vector.tensor_scalar(
                    out=pairwise(tt), in0=t["y01"], scalar1=1.0 / (2.0 * math.pi), scalar2=0.25,
                    op0=ALU.mult, op1=ALU.add,
                )
            t["t0"] = tt[:, 0]
            t["t1"] = tt[:, 1]

        def whole_turns(t):
            whole = work.tile([P, E], F32, name="whole")
            nc.vector.tensor_scalar(
                out=whole[:], in0=t["t1"], scalar1=ROUND_MAGIC, scalar2=ROUND_MAGIC,
                op0=ALU.add, op1=ALU.subtract,
            )
            t["whole"] = whole

        def fraction(t):
            frac = ready.tile([P, E], F32, name="frac")
            nc.vector.tensor_tensor(out=frac[:], in0=t["t1"], in1=t["whole"][:], op=ALU.subtract)
            t["frac"] = frac

        def scalar_tanh0(t):
            th = work.tile([P, E], F32, name="th0")
            nc.scalar.activation(
                out=th[:], in_=t["t0"], func=ACT.Tanh, scale=2.0 * math.pi, bias=-0.5 * math.pi
            )
            t["th0"] = th

        def scalar_sq0(t):
            sq = late.tile([P, E], F32, name="sq0")
            nc.scalar.activation(out=sq[:], in_=t["th0"][:], func=ACT.Square)
            t["sq0"] = sq

        def scalar_cos(t):
            cos_y = late.tile([P, E], F32, name="cos_y")
            nc.scalar.activation(out=cos_y[:], in_=t["frac"][:], func=ACT.Sin, scale=2.0 * math.pi)
            t["cos"] = cos_y

        def group_g(t):
            words = late.tile([P, KINDS * E], BF16, name="g_words")
            nc.vector.tensor_copy(
                out=words[:].bitcast(F32).rearrange("p (hi m j) -> p m hi j", hi=2, j=PACK),
                in_=t["g_raw"][:].bitcast(F32).rearrange("p (j m hi) -> p m hi j", j=PACK, hi=2),
            )
            for kind in range(KINDS):
                first = (kind // 2) * 2 * E + kind % 2
                t["g", kind] = words[:, first : first + 2 * E - 1 : 2]

        def group_x(t, first, last, copy):
            copy(
                out=t["x_grouped"][:, first:last, :].rearrange("p (r i) j -> p r j i", i=4),
                in_=t["x"][:, :, first:last].rearrange("p j (r i) -> p r j i", i=4),
            )

        def scalar_x(t):
            t["x_grouped"] = xg_pool.tile([P, IN_F, PACK], BF16, align_bytes=64, name="x_grouped")
            group_x(t, X_VECTOR_COLS, IN_F, nc.scalar.copy)

        def vector_x(t):
            group_x(t, 0, X_VECTOR_COLS, nc.vector.tensor_copy)

        def quantise_x(t, c, n):
            n_cols = slice(n * N_TILE, (n + 1) * N_TILE)
            nc.vector.quantize_mx(
                out=x_codes[:, c, n_cols].bitcast(E4M3X4),
                scales=x_scales[:, c, n_cols],
                in_=t["x_grouped"][:, n_cols, :].rearrange("p col j -> p (col j)"),
            )

        def times_grad(t, kind, group):
            s = group.index(kind)
            if ("dy", group) not in t:
                t["dy", group] = dy_pool.tile([P, len(group), E], BF16, align_bytes=64, name="dy")
            dy = t["dy", group]
            if kind == 2:
                nc.vector.scalar_tensor_tensor(
                    out=dy[:, s], in0=t["th2"], scalar=0.0, in1=t["g", 2], op0=ALU.is_gt, op1=ALU.mult
                )
            elif kind == 1:
                nc.vector.tensor_tensor(out=dy[:, s], in0=t["cos"][:], in1=t["g", 1], op=ALU.mult)
            else:
                nc.vector.scalar_tensor_tensor(
                    out=dy[:, s], in0=t["sq%d" % kind][:], scalar=1.0, in1=t["g", kind],
                    op0=ALU.subtract, op1=ALU.mult,
                )

        def stage_g(t):
            for b, pair in enumerate((A, B)):
                bank = psum.tile([P, 2, E], BF16, name="acc1%d" % b)
                for s, kind in enumerate(pair):
                    nc.tensor.matmul(
                        out=bank[:, s].rearrange("p (m j) -> p m j", j=PACK),
                        lhsT=ident[:],
                        rhs=t["g_raw"][:].rearrange("p (j m k) -> p k m j", j=PACK, k=KINDS)[:, kind],
                        start=True,
                        stop=True,
                    )
                    t["g", kind] = bank[:, s]

        def quantise_dy(t, pair, kept):
            pool = late if kept else dy_pool
            codes = pool.tile([P, len(pair), M], U32, align_bytes=64, name="dy_codes")
            scales = pool.tile([P, len(pair), M], U8, align_bytes=64, name="dy_scales")
            nc.vector.quantize_mx(
                out=codes[:].rearrange("p s m -> p (s m)").bitcast(E5M2X4),
                scales=scales[:].rearrange("p s m -> p (s m)"),
                in_=t["dy", pair][:].rearrange("p s e -> p (s e)"),
            )
            t["codes", pair] = codes
            t["scales", pair] = scales

        acc = {}

        def products(t, i, pair):
            h, c = divmod(i, PASSES)
            for s, kind in enumerate(pair):
                for n in range(N_TILES):
                    if c == 0:
                        acc[kind, n] = psum.tile([P, N_TILE], F32, name="acc%d%d" % (kind, n))
                    n_cols = slice(n * N_TILE, (n + 1) * N_TILE)
                    nc.tensor.matmul_mx(
                        out=acc[kind, n][:],
                        lhsT=t["codes", pair][:, s].bitcast(E5M2X4),
                        lhsT_scale=t["scales", pair][:, s],
                        rhs=x_codes[:, c, n_cols].bitcast(E4M3X4),
                        rhs_scale=x_scales[:, c, n_cols],
                        start=(c == 0),
                        stop=(c == PASSES - 1),
                    )

        def send_out(h, kind, n, by_vector):
            result = stage.tile([P, N_TILE], F32, name="result")
            if by_vector:
                nc.vector.tensor_scalar_mul(out=result[:], in0=acc[kind, n][:], scalar1=SIGN[kind])
            else:
                nc.scalar.mul(out=result[:], in_=acc[kind, n][:], mul=SIGN[kind])
            nc.sync.dma_start(out=out_rows[h, kind][:, n * N_TILE : (n + 1) * N_TILE], in_=result[:])

        zero = keep.tile([P, 1], F32)
        unused = keep.tile([P, 1], F32)
        nc.vector.memset(zero[:], 0.0)
        nc.scalar.activation(out=unused[:], in_=zero[:], func=ACT.Silu)

        chunks = {}

        def run(step):
            name, i = step[0], step[1]
            if name == "load":
                chunks[i] = load(i)
                return
            if name == "out":
                send_out(i, step[2], step[3], step[4])
                return
            t = chunks[i]
            if name == "loadx": load_x(t, i)
            elif name == "th23": scalar_23(t)
            elif name == "sq3": scalar_sq3(t)
            elif name == "th0": scalar_tanh0(t)
            elif name == "sq0": scalar_sq0(t)
            elif name == "cos": scalar_cos(t)
            elif name == "sx": scalar_x(t)
            elif name == "turns": turns(t, False)
            elif name == "whole": whole_turns(t)
            elif name == "frac": fraction(t)
            elif name == "gg": group_g(t)
            elif name == "gx": vector_x(t)
            elif name == "qx": quantise_x(t, i, step[2])
            elif name == "stt": times_grad(t, step[2], group_of(i, step[2]))
            elif name == "q": quantise_dy(t, step[2], i < PASSES and step[2] == (1,))
            elif name == "stage": stage_g(t)
            elif name == "mm": products(t, i, step[2])
            else: assert False, name

        def needs(step):
            name, i = step[0], step[1]
            if name == "load":
                k = i - YG_BUFS
                return [("th23", k), ("turns", k), ("stage" if k < PASSES else "gg", k)] if k >= 0 else []
            if name == "loadx":
                k = i - X_BUFS
                return [("load", i)] + ([("sx", k), ("gx", k)] if k >= 0 else [])
            if name == "out":
                return [("mm", i * PASSES + PASSES - 1, group_of(i * PASSES, step[2]))]
            if name == "mm":
                h, c = divmod(i, PASSES)
                req = [("q", i, step[2]), ("qx", c, 0), ("qx", c, 1)]
                if i == 0 and step[2] == (1,):
                    req += [("stt", PASSES - 1, kind) for kind in range(KINDS)]
                if h == 1 and c == 0:
                    req += [("out", 0, kind, n) for kind in step[2] for n in range(N_TILES)]
                return req
            table = {
                "th23": ["load"], "turns": ["load"], "gg": ["load"], "sx": ["loadx"], "gx": ["sx"],
                "sq3": ["th23"], "th0": ["turns"], "sq0": ["th0"], "whole": ["turns"], "frac": ["whole"],
                "cos": ["frac"],
            }
            turn = {
                "th23": (3, [("sq3",), ("stt", 2), ("stt", 3)]), "turns": (3, [("th0",), ("frac",)]),
                "whole": (2, [("frac",)]), "frac": (3, [("cos",)]), "th0": (2, [("sq0",)]),
                "sq0": (PASSES + 2, [("stt", 0)]), "cos": (PASSES + 2, [("stt", 1)]),
                "gg": (PASSES + 2, [("stt", 0), ("stt", 1), ("stt", 2), ("stt", 3)]),
                "sx": (2, [("qx", 0), ("qx", 1)]),
            }
            old = []
            if name in turn and i - turn[name][0] >= 0:
                old = [(r[0], i - turn[name][0]) + r[1:] for r in turn[name][1]]
            if name in table:
                return old + [(a, i) for a in table[name]]
            if name == "qx":
                return [("gx", i), ("sx", i)]
            if name == "stage":
                return [("load", i)] + ([("stt", i - 1, kind) for kind in range(KINDS)] if i else [])
            if name == "stt":
                made = ("th23", "cos", "th23", "sq3")[step[2]] if step[2] else "sq0"
                return [(made, i), ("stage" if i < PASSES else "gg", i)]
            if name == "q":
                mine = [s for s in queues[3] if s[0] == "mm" and not (s[1] < PASSES and s[2] == (1,))]
                k = mine.index(("mm", i, step[2])) - DY_BUFS if ("mm", i, step[2]) in mine else -1
                return [("stt", i, kind) for kind in step[2]] + ([mine[k]] if k >= 0 else [])
            assert False, name

        queues = program()
        at = [0 for q in queues]
        done = set()
        left = sum(len(q) for q in queues)
        while left:
            moved = False
            for k, q in enumerate(queues):
                while at[k] < len(q) and all(r in done for r in needs(q[at[k]])):
                    step = q[at[k]]
                    run(step)
                    done.add(step[:4] if step[0] == "out" else step)
                    at[k] += 1
                    left -= 1
                    moved = True
            assert moved, [q[at[k]] for k, q in enumerate(queues) if at[k] < len(q)]
